import numpy as np
import ml_dtypes


def mxq(x, axis, fmt="e4m3"):
    dtype, down = {"e4m3": (ml_dtypes.float8_e4m3fn, 7), "e5m2": (ml_dtypes.float8_e5m2, 14)}[fmt]
    v = np.moveaxis(np.asarray(x, np.float32).astype(ml_dtypes.bfloat16).astype(np.float64), axis, -1)
    blocks = v.reshape(v.shape[:-1] + (-1, 32))
    amax = np.abs(blocks).max(-1, keepdims=True)
    byte = np.maximum(np.where(amax > 0, np.frexp(amax)[1] - 1 + 127, 0) - down, 1)
    scale = np.exp2(byte - 127.0)
    codes = (blocks / scale).astype(np.float32).astype(dtype).astype(np.float64)
    return np.moveaxis((codes * scale).reshape(v.shape), -1, axis)


WIDE = False


def mx_kscale(k):
    if not WIDE:
        return np.ones(k)
    levels = np.array([10, -10, 5, -5, 0])
    a = np.random.permutation(np.resize(levels, k // 512 * 4)).reshape(k // 512, 4)
    idx = np.arange(k)
    return np.exp2(a[idx // 512, idx % 128 // 32])


BF16 = ml_dtypes.bfloat16


def bf(x):
    return np.asarray(x, np.float32).astype(BF16)


def f64(x):
    return np.asarray(x).astype(np.float64)


B, N, D, O, G, STEPS = 3, 512, 512, 512, 5, 3
R = B * N
J = G * O


def signed_sqrt(x):
    ax = np.abs(x)
    safe = np.where(ax > 0, ax, 1.0)
    return np.sign(x) * np.sqrt(safe)


def setup_inputs():
    s = mx_kscale(D)
    return {"h": bf(np.random.standard_normal((R, D)) / np.sqrt(D) * s),
            "neighbours": bf(np.random.standard_normal((R, D)) * 1.5 * s),
            "W_node": bf(np.random.standard_normal((D, J)) / s[:, None]),
            "b_node": bf(np.random.standard_normal(J) * 0.1),
            "W_nb": bf(np.random.standard_normal((D, J)) / np.sqrt(D) / s[:, None]),
            "b_nb": bf(np.random.standard_normal(J) * 0.3)}


def reference(h, neighbours, W_node, b_node, W_nb, b_nb):
    data_out = (mxq(f64(h), 1, "e4m3") @ mxq(f64(W_node), 0, "e4m3")) + f64(b_node)
    img_feat = (mxq(f64(neighbours), 1, "e4m3") @ mxq(f64(W_nb), 0, "e4m3")) + f64(b_nb)
    iq = data_out * img_feat
    iq = iq.reshape(-1, O, G).sum(axis=2)
    iq = signed_sqrt(iq)
    norm = np.sqrt(np.sum(iq * iq, axis=1, keepdims=True))
    return iq / np.maximum(norm, 1e-12)

@@ -1,0 +1,218 @@
+from contextlib import ExitStack
+
+import concourse.mybir as mybir
+from concourse.masks import make_identity
+
+F32 = mybir.dt.float32
+BF16 = mybir.dt.bfloat16
+U32 = mybir.dt.uint32
+U8 = mybir.dt.uint8
+FP8X4 = mybir.dt.float8_e4m3fn_x4
+ACT = mybir.ActivationFunctionType
+ALU = mybir.AluOpType
+
+P = 128
+R, D, O, G = 1536, 512, 512, 5
+J = O * G
+RT = 512
+N_RT = R // RT
+N_OB = O // P
+A = RT // P
+CH = P * G
+FLOPS = 2 * 2 * R * D * J
+BIG = 1.0e19
+TAIL_AT = 2
+
+
+def tile_gnn_new_pb_kernel(tc, h, neighbours, W_node, b_node, W_nb, b_nb, out):
+    nc = tc.nc
+    acts = (h, neighbours)
+    weights = (W_node, W_nb)
+    with ExitStack() as ctx:
+        keep = ctx.enter_context(tc.tile_pool(name="keep", bufs=1))
+        stage = ctx.enter_context(tc.tile_pool(name="stage", bufs=3))
+        upool = ctx.enter_context(tc.tile_pool(name="upool", bufs=4))
+        ppool = ctx.enter_context(tc.tile_pool(name="ppool", bufs=10))
+        wpool = ctx.enter_context(tc.tile_pool(name="wpool", bufs=2))
+        pu = ctx.enter_context(tc.psum_pool(name="pu", bufs=3))
+        pv = ctx.enter_context(tc.psum_pool(name="pv", bufs=4))
+        pz = ctx.enter_context(tc.psum_pool(name="pz", bufs=1))
+
+        xraw = [[keep.tile([P, A * D], BF16, name="xraw%d%d" % (x, rt)) for rt in range(N_RT)] for x in range(2)]
+        wraw = [keep.tile([P, 4, J], BF16, name="wraw%d" % w) for w in range(2)]
+        xc = [keep.tile([P, R], U32, name="xc%d" % x, align_bytes=64) for x in range(2)]
+        xs = [keep.tile([P, R], U8, name="xs%d" % x, align_bytes=64) for x in range(2)]
+        wc = [keep.tile([P, J], U32, name="wc%d" % w, align_bytes=64) for w in range(2)]
+        ws = [keep.tile([P, J], U8, name="ws%d" % w, align_bytes=64) for w in range(2)]
+        y = keep.tile([P, N_RT, A, O], F32, name="y")
+        ident = keep.tile([P, P], F32, name="ident")
+        braw = keep.tile([P, CH], BF16, name="braw")
+        bf = keep.tile([P, G, P], F32, name="bf")
+        bias_t = keep.tile([P, G, 8], F32, name="bias_t")
+        one = keep.tile([P, 1], F32, name="one")
+        warm = keep.tile([P, 1], F32, name="warm")
+        ssum = keep.tile([P, N_RT * A], F32, name="ssum")
+        rn_raw = keep.tile([P, N_RT * A], F32, name="rn_raw")
+        rn = keep.tile([P, N_RT * A], F32, name="rn")
+
+        nc.vector.memset(braw[:], 0.0)
+        nc.vector.memset(one[:], 1.0)
+        make_identity(nc, ident[:])
+        nc.scalar.activation(out=warm[:], in_=one[:], func=ACT.Abs_reciprocal_sqrt)
+
+        def load_x(x, rt):
+            nc.sync.dma_start(
+                out=xraw[x][rt][:],
+                in_=acts[x][rt * RT:(rt + 1) * RT, :].rearrange("(p a) k -> p (a k)", a=A),
+            )
+
+        def load_w(w, ob):
+            for u in range(2):
+                nc.sync.dma_start(
+                    out=wraw[w][:, 2 * u:2 * u + 2, ob * CH:(ob + 1) * CH],
+                    in_=weights[w][256 * u:256 * u + 256, ob * CH:(ob + 1) * CH].rearrange("(q e) c -> q e c", e=2),
+                )
+
+        nc.scalar.dma_start(out=braw[0:4, :], in_=b_node.rearrange("(o c) -> o c", o=N_OB))
+        nc.scalar.dma_start(out=braw[4:8, :], in_=b_nb.rearrange("(o c) -> o c", o=N_OB))
+        load_x(0, 0)
+        load_w(0, 0)
+        load_x(1, 0)
+        load_w(1, 0)
+        for rt in range(1, N_RT):
+            load_x(0, rt)
+            load_x(1, rt)
+        for ob in range(1, N_OB):
+            load_w(0, ob)
+            load_w(1, ob)
+
+        nc.vector.tensor_copy(out=bf[:], in_=braw[:].rearrange("p (m g) -> p g m", g=G))
+        bt0 = pv.tile([P, 512], F32, tag="v")
+        for g in range(4):
+            nc.tensor.transpose(bt0[:, g * P:(g + 1) * P], bf[:, g, :], ident[:])
+        nc.vector.tensor_copy(out=bias_t[:, 0:4, :], in_=bt0[:].rearrange("p (g r) -> p g r", g=4)[:, :, 0:8])
+        bt1 = pv.tile([P, 512], F32, tag="v")
+        nc.tensor.transpose(bt1[:, 0:P], bf[:, 4, :], ident[:])
+        nc.vector.tensor_copy(out=bias_t[:, 4, :], in_=bt1[:, 0:8])
+
+        def prep_x(x, rt):
+            grouped = stage.tile([P, 4 * RT], BF16, tag="xg", align_bytes=64)
+            g32 = grouped[:].bitcast(F32).rearrange("q (a c u) -> q a c u", a=A, u=2)
+            r32 = xraw[x][rt][:].bitcast(F32)
+            for half in range(2):
+                pool = pu if half == 0 else pv
+                t = pool.tile([P, 512], F32, tag="u" if half == 0 else "v")
+                for i in range(4):
+                    col = half * 512 + i * P
+                    nc.tensor.transpose(t[:, i * P:(i + 1) * P], r32[:, col:col + P], ident[:])
+                nc.scalar.copy(
+                    out=g32[:, 2 * half:2 * half + 2],
+                    in_=t[:].rearrange("q (a u c) -> q a c u", a=2, u=2),
+                )
+            nc.vector.quantize_mx(
+                out=xc[x][:, rt * RT:(rt + 1) * RT].bitcast(FP8X4),
+                scales=xs[x][:, rt * RT:(rt + 1) * RT],
+                in_=grouped[:],
+            )
+
+        def prep_w(w, ob):
+            src = wraw[w][:, :, ob * CH:(ob + 1) * CH].rearrange("q t (m g) -> q g m t", g=G)
+            g4 = stage.tile([P, 4, P, 4], BF16, tag="g4", align_bytes=64)
+            nc.vector.tensor_copy(out=g4[:], in_=src[:, 0:4])
+            g1 = stage.tile([P, P, 4], BF16, tag="g1", align_bytes=64)
+            nc.scalar.copy(out=g1[:], in_=src[:, 4])
+            c0 = ob * CH
+            nc.vector.quantize_mx(
+                out=wc[w][:, c0:c0 + 512].bitcast(FP8X4),
+                scales=ws[w][:, c0:c0 + 512],
+                in_=g4[:].rearrange("q g m t -> q (g m t)"),
+            )
+            nc.vector.quantize_mx(
+                out=wc[w][:, c0 + 512:c0 + CH].bitcast(FP8X4),
+                scales=ws[w][:, c0 + 512:c0 + CH],
+                in_=g1[:].rearrange("q m t -> q (m t)"),
+            )
+
+        def passes(ob, rt, g):
+            c0 = (ob * G + g) * P
+            banks = []
+            for w in range(2):
+                pool = pu if w == 0 else pv
+                bank = pool.tile([P, RT], F32, tag="u" if w == 0 else "v")
+                nc.tensor.matmul_mx(
+                    out=bank[:],
+                    lhsT=wc[w][:, c0:c0 + P].bitcast(FP8X4),
+                    lhsT_scale=ws[w][:, c0:c0 + P],
+                    rhs=xc[w][:, rt * RT:(rt + 1) * RT].bitcast(FP8X4),
+                    rhs_scale=xs[w][:, rt * RT:(rt + 1) * RT],
+                    start=True,
+                    stop=True,
+                )
+                banks.append(bank)
+            u_sb = upool.tile([P, RT], F32, tag="usb")
+            nc.scalar.activation(out=u_sb[:], in_=banks[0][:], func=ACT.Identity,
+                                 bias=bias_t[:, g, ob:ob + 1], scale=1.0)
+            prod = ppool.tile([P, RT], F32, tag="p")
+            nc.vector.scalar_tensor_tensor(out=prod[:], in0=banks[1][:], scalar=bias_t[:, g, 4 + ob:5 + ob],
+                                           in1=u_sb[:], op0=ALU.add, op1=ALU.mult)
+            return prod
+
+        def pool_and_root(ob, rt, prods):
+            z = pz.tile([P, A, P], F32, tag="z")
+            for a in range(A):
+                for g in range(G):
+                    nc.tensor.matmul(out=z[:, a, :], lhsT=prods[g][:, a * P:(a + 1) * P], rhs=ident[:],
+                                     start=(g == 0), stop=(g == G - 1), is_transpose=True)
+            w_sb = wpool.tile([P, A, P], F32, tag="w")
+            nc.scalar.activation(out=w_sb[:], in_=z[:], func=ACT.Abs_reciprocal_sqrt)
+            nc.vector.scalar_tensor_tensor(out=y[:, rt, :, ob * P:(ob + 1) * P], in0=w_sb[:], scalar=BIG,
+                                           in1=z[:], op0=ALU.min, op1=ALU.mult)
+
+        out_v = out.rearrange("(t p a) o -> t p a o", t=N_RT, a=A)
+
+        def finish(rt):
+            cols = slice(rt * A, (rt + 1) * A)
+            for a in range(A):
+                junk = wpool.tile([P, O], F32, tag="junk")
+                nc.scalar.activation(out=junk[:], in_=y[:, rt, a, :], func=ACT.Square,
+                                     accum_out=ssum[:, rt * A + a:rt * A + a + 1])
+            nc.scalar.activation(out=rn_raw[:, cols], in_=ssum[:, cols], func=ACT.Abs_reciprocal_sqrt)
+            nc.vector.tensor_scalar_min(out=rn[:, cols], in0=rn_raw[:, cols], scalar1=1.0e12)
+            last = rt == N_RT - 1
+            for a in range(A):
+                sc = rn[:, rt * A + a:rt * A + a + 1]
+                if last and a < 2:
+                    nc.vector.tensor_scalar_mul(out=y[:, rt, a, :], in0=y[:, rt, a, :], scalar1=sc)
+                elif last and a == 2:
+                    nc.scalar.activation(out=y[:, rt, a, :], in_=y[:, rt, a, :], func=ACT.Copy, scale=sc)
+                else:
+                    nc.gpsimd.tensor_scalar(out=y[:, rt, a, :], in0=y[:, rt, a, :], scalar1=sc, scalar2=0.0,
+                                            op0=ALU.mult, op1=ALU.add)
+                if last:
+                    nc.sync.dma_start(out=out_v[rt][:, a, :], in_=y[:, rt, a, :])
+            if not last:
+                nc.sync.dma_start(out=out_v[rt], in_=y[:, rt])
+
+        prep_x(0, 0)
+        prep_w(0, 0)
+        prep_x(1, 0)
+        prep_w(1, 0)
+        pending = None
+        for ob in range(N_OB):
+            for rt in range(N_RT):
+                prods = []
+                for g in range(G):
+                    prods.append(passes(ob, rt, g))
+                    if g == TAIL_AT and pending is not None:
+                        pool_and_root(*pending)
+                        if pending[0] == N_OB - 1:
+                            finish(pending[1])
+                pending = (ob, rt, prods)
+                if ob == 0 and rt + 1 < N_RT:
+                    prep_x(0, rt + 1)
+                    prep_x(1, rt + 1)
+                if rt == 0 and ob + 1 < N_OB:
+                    prep_w(0, ob + 1)
+                    prep_w(1, ob + 1)
+        pool_and_root(*pending)
+        finish(pending[1])

@@ -21,7 +21,25 @@ A = RT // P
 CH = P * G
 FLOPS = 2 * 2 * R * D * J
 BIG = 1.0e19
-TAIL_AT = 2
+PU = 3
+PV = 3
+PZ = 2
+VLAG = 2
+T_AT = 0
+S_AT = 0
+V_AT = 1
+Q_AT = 2
+Q_STEP = 0
+F_AT = 1
+HEAD_ENG = "VVSSS"
+BODY_ENG = ("GGGGV", "GGGGG")
+ADDS = 1
+X_AT = (0, 1)
+X_LAG = 1
+X_ENG = "SS"
+W_AT = 1
+W_STEP = 13
+W_LAG = 3
 
 
 def tile_gnn_new_pb_kernel(tc, h, neighbours, W_node, b_node, W_nb, b_nb, out):
@@ -30,35 +48,32 @@ def tile_gnn_new_pb_kernel(tc, h, neighbours, W_node, b_node, W_nb, b_nb, out):
     weights = (W_node, W_nb)
     with ExitStack() as ctx:
         keep = ctx.enter_context(tc.tile_pool(name="keep", bufs=1))
-        stage = ctx.enter_context(tc.tile_pool(name="stage", bufs=3))
-        upool = ctx.enter_context(tc.tile_pool(name="upool", bufs=4))
-        ppool = ctx.enter_context(tc.tile_pool(name="ppool", bufs=10))
-        wpool = ctx.enter_context(tc.tile_pool(name="wpool", bufs=2))
-        pu = ctx.enter_context(tc.psum_pool(name="pu", bufs=3))
-        pv = ctx.enter_context(tc.psum_pool(name="pv", bufs=4))
-        pz = ctx.enter_context(tc.psum_pool(name="pz", bufs=1))
+        xstage = ctx.enter_context(tc.tile_pool(name="xstage", bufs=3))
+        wstage = ctx.enter_context(tc.tile_pool(name="wstage", bufs=4))
+        upool = ctx.enter_context(tc.tile_pool(name="upool", bufs=6))
+        ppool = ctx.enter_context(tc.tile_pool(name="ppool", bufs=12))
+        apool = ctx.enter_context(tc.tile_pool(name="apool", bufs=4))
+        rpool = ctx.enter_context(tc.tile_pool(name="rpool", bufs=2))
+        pu = ctx.enter_context(tc.psum_pool(name="pu", bufs=PU))
+        pv = ctx.enter_context(tc.psum_pool(name="pv", bufs=PV))
+        pz = ctx.enter_context(tc.psum_pool(name="pz", bufs=PZ))
 
         xraw = [[keep.tile([P, A * D], BF16, name="xraw%d%d" % (x, rt)) for rt in range(N_RT)] for x in range(2)]
-        wraw = [keep.tile([P, 4, J], BF16, name="wraw%d" % w) for w in range(2)]
-        xc = [keep.tile([P, R], U32, name="xc%d" % x, align_bytes=64) for x in range(2)]
-        xs = [keep.tile([P, R], U8, name="xs%d" % x, align_bytes=64) for x in range(2)]
-        wc = [keep.tile([P, J], U32, name="wc%d" % w, align_bytes=64) for w in range(2)]
-        ws = [keep.tile([P, J], U8, name="ws%d" % w, align_bytes=64) for w in range(2)]
-        y = keep.tile([P, N_RT, A, O], F32, name="y")
+        wraw = [[keep.tile([P, 4, CH], BF16, name="wraw%d%d" % (w, ob)) for ob in range(N_OB)] for w in range(2)]
+        xc = [[keep.tile([P, RT], U32, name="xc%d%d" % (x, rt), align_bytes=64) for rt in range(N_RT)] for x in range(2)]
+        xs = [[keep.tile([P, RT], U8, name="xs%d%d" % (x, rt), align_bytes=64) for rt in range(N_RT)] for x in range(2)]
+        wc = [[keep.tile([P, CH], U32, name="wc%d%d" % (w, ob), align_bytes=64) for ob in range(N_OB)] for w in range(2)]
+        ws = [[keep.tile([P, CH], U8, name="ws%d%d" % (w, ob), align_bytes=64) for ob in range(N_OB)] for w in range(2)]
+        y = [keep.tile([P, A, O], F32, name="y%d" % rt) for rt in range(N_RT)]
         ident = keep.tile([P, P], F32, name="ident")
-        braw = keep.tile([P, CH], BF16, name="braw")
-        bf = keep.tile([P, G, P], F32, name="bf")
-        bias_t = keep.tile([P, G, 8], F32, name="bias_t")
+        bias_t = [keep.tile([P, N_OB, 6], BF16, name="bias%d" % w) for w in range(2)]
         one = keep.tile([P, 1], F32, name="one")
         warm = keep.tile([P, 1], F32, name="warm")
-        ssum = keep.tile([P, N_RT * A], F32, name="ssum")
-        rn_raw = keep.tile([P, N_RT * A], F32, name="rn_raw")
-        rn = keep.tile([P, N_RT * A], F32, name="rn")
+        part = [[keep.tile([P, A], F32, name="part%d%d" % (rt, k)) for k in range(3)] for rt in range(N_RT)]
+        ssum = [keep.tile([P, A], F32, name="ssum%d" % rt) for rt in range(N_RT)]
+        rn = [keep.tile([P, A], F32, name="rn%d" % rt) for rt in range(N_RT)]
 
-        nc.vector.memset(braw[:], 0.0)
-        nc.vector.memset(one[:], 1.0)
-        make_identity(nc, ident[:])
-        nc.scalar.activation(out=warm[:], in_=one[:], func=ACT.Abs_reciprocal_sqrt)
+        ctx.enter_context(tc.manual_schedule())
 
         def load_x(x, rt):
             nc.sync.dma_start(
@@ -69,150 +84,249 @@ def tile_gnn_new_pb_kernel(tc, h, neighbours, W_node, b_node, W_nb, b_nb, out):
         def load_w(w, ob):
             for u in range(2):
                 nc.sync.dma_start(
-                    out=wraw[w][:, 2 * u:2 * u + 2, ob * CH:(ob + 1) * CH],
+                    out=wraw[w][ob][:, 2 * u:2 * u + 2, :],
                     in_=weights[w][256 * u:256 * u + 256, ob * CH:(ob + 1) * CH].rearrange("(q e) c -> q e c", e=2),
                 )
 
-        nc.scalar.dma_start(out=braw[0:4, :], in_=b_node.rearrange("(o c) -> o c", o=N_OB))
-        nc.scalar.dma_start(out=braw[4:8, :], in_=b_nb.rearrange("(o c) -> o c", o=N_OB))
+        nc.vector.memset(one[:], 1.0)
         load_x(0, 0)
         load_w(0, 0)
         load_x(1, 0)
         load_w(1, 0)
+        for w, b in enumerate((b_node, b_nb)):
+            nc.sync.dma_start(out=bias_t[w][:, :, 0:G], in_=b.rearrange("(o m g) -> m o g", o=N_OB, g=G))
         for rt in range(1, N_RT):
             load_x(0, rt)
             load_x(1, rt)
         for ob in range(1, N_OB):
             load_w(0, ob)
             load_w(1, ob)
+        make_identity(nc, ident[:])
+        nc.scalar.activation(out=warm[:], in_=one[:], func=ACT.Abs_reciprocal_sqrt)
 
-        nc.vector.tensor_copy(out=bf[:], in_=braw[:].rearrange("p (m g) -> p g m", g=G))
-        bt0 = pv.tile([P, 512], F32, tag="v")
-        for g in range(4):
-            nc.tensor.transpose(bt0[:, g * P:(g + 1) * P], bf[:, g, :], ident[:])
-        nc.vector.tensor_copy(out=bias_t[:, 0:4, :], in_=bt0[:].rearrange("p (g r) -> p g r", g=4)[:, :, 0:8])
-        bt1 = pv.tile([P, 512], F32, tag="v")
-        nc.tensor.transpose(bt1[:, 0:P], bf[:, 4, :], ident[:])
-        nc.vector.tensor_copy(out=bias_t[:, 4, :], in_=bt1[:, 0:8])
+        xg = {}
 
-        def prep_x(x, rt):
-            grouped = stage.tile([P, 4 * RT], BF16, tag="xg", align_bytes=64)
+        def turn_x(x, rt, engines):
+            grouped = xstage.tile([P, 4 * RT], BF16, tag="xg", align_bytes=64)
+            xg[x, rt] = grouped
             g32 = grouped[:].bitcast(F32).rearrange("q (a c u) -> q a c u", a=A, u=2)
             r32 = xraw[x][rt][:].bitcast(F32)
             for half in range(2):
-                pool = pu if half == 0 else pv
-                t = pool.tile([P, 512], F32, tag="u" if half == 0 else "v")
+                t = pz.tile([P, 512], F32, tag="z")
                 for i in range(4):
                     col = half * 512 + i * P
                     nc.tensor.transpose(t[:, i * P:(i + 1) * P], r32[:, col:col + P], ident[:])
-                nc.scalar.copy(
-                    out=g32[:, 2 * half:2 * half + 2],
-                    in_=t[:].rearrange("q (a u c) -> q a c u", a=2, u=2),
-                )
+                dst = g32[:, 2 * half:2 * half + 2]
+                src = t[:].rearrange("q (a u c) -> q a c u", a=2, u=2)
+                if engines[half] == "S":
+                    nc.scalar.copy(out=dst, in_=src)
+                else:
+                    nc.vector.tensor_copy(out=dst, in_=src)
+
+        def quant_x(x, rt):
+            nc.vector.quantize_mx(out=xc[x][rt][:].bitcast(FP8X4), scales=xs[x][rt][:], in_=xg[x, rt][:])
+
+        wg = {}
+
+        def regroup_w(w, ob, g, engine):
+            if g == 0:
+                grouped = wstage.tile([P, G, P, 4], BF16, tag="wg", align_bytes=64)
+                wg[w, ob] = grouped
+            dst = wg[w, ob][:, g]
+            src = wraw[w][ob][:].rearrange("q t (m g) -> q g m t", g=G)[:, g]
+            if engine == "S":
+                nc.scalar.copy(out=dst, in_=src)
+            elif engine == "V":
+                nc.vector.tensor_copy(out=dst, in_=src)
+            else:
+                nc.gpsimd.tensor_scalar(out=dst, in0=src, scalar1=1.0, scalar2=0.0, op0=ALU.mult, op1=ALU.add)
+
+        def quant_w(w, ob, g0, n):
+            cols = slice(g0 * P, (g0 + n) * P)
             nc.vector.quantize_mx(
-                out=xc[x][:, rt * RT:(rt + 1) * RT].bitcast(FP8X4),
-                scales=xs[x][:, rt * RT:(rt + 1) * RT],
-                in_=grouped[:],
+                out=wc[w][ob][:, cols].bitcast(FP8X4),
+                scales=ws[w][ob][:, cols],
+                in_=wg[w, ob][:, g0:g0 + n].rearrange("q g m t -> q (g m t)"),
             )
 
-        def prep_w(w, ob):
-            src = wraw[w][:, :, ob * CH:(ob + 1) * CH].rearrange("q t (m g) -> q g m t", g=G)
-            g4 = stage.tile([P, 4, P, 4], BF16, tag="g4", align_bytes=64)
-            nc.vector.tensor_copy(out=g4[:], in_=src[:, 0:4])
-            g1 = stage.tile([P, P, 4], BF16, tag="g1", align_bytes=64)
-            nc.scalar.copy(out=g1[:], in_=src[:, 4])
-            c0 = ob * CH
-            nc.vector.quantize_mx(
-                out=wc[w][:, c0:c0 + 512].bitcast(FP8X4),
-                scales=ws[w][:, c0:c0 + 512],
-                in_=g4[:].rearrange("q g m t -> q (g m t)"),
+        def one_pass(w, ob, rt, g):
+            cols = slice(g * P, (g + 1) * P)
+            pool = pu if w == 0 else pv
+            bank = pool.tile([P, RT], F32, tag="u" if w == 0 else "v")
+            nc.tensor.matmul_mx(
+                out=bank[:],
+                lhsT=wc[w][ob][:, cols].bitcast(FP8X4),
+                lhsT_scale=ws[w][ob][:, cols],
+                rhs=xc[w][rt][:].bitcast(FP8X4),
+                rhs_scale=xs[w][rt][:],
+                start=True,
+                stop=True,
             )
-            nc.vector.quantize_mx(
-                out=wc[w][:, c0 + 512:c0 + CH].bitcast(FP8X4),
-                scales=ws[w][:, c0 + 512:c0 + CH],
-                in_=g1[:].rearrange("q m t -> q (m t)"),
-            )
+            return bank
 
-        def passes(ob, rt, g):
-            c0 = (ob * G + g) * P
-            banks = []
-            for w in range(2):
-                pool = pu if w == 0 else pv
-                bank = pool.tile([P, RT], F32, tag="u" if w == 0 else "v")
-                nc.tensor.matmul_mx(
-                    out=bank[:],
-                    lhsT=wc[w][:, c0:c0 + P].bitcast(FP8X4),
-                    lhsT_scale=ws[w][:, c0:c0 + P],
-                    rhs=xc[w][:, rt * RT:(rt + 1) * RT].bitcast(FP8X4),
-                    rhs_scale=xs[w][:, rt * RT:(rt + 1) * RT],
-                    start=True,
-                    stop=True,
-                )
-                banks.append(bank)
+        def take_u(ob, g, bank):
             u_sb = upool.tile([P, RT], F32, tag="usb")
-            nc.scalar.activation(out=u_sb[:], in_=banks[0][:], func=ACT.Identity,
-                                 bias=bias_t[:, g, ob:ob + 1], scale=1.0)
+            nc.scalar.activation(out=u_sb[:], in_=bank[:], func=ACT.Identity,
+                                 bias=bias_t[0][:, ob, g:g + 1], scale=1.0)
+            return u_sb
+
+        def product(ob, g, bank, u_sb):
             prod = ppool.tile([P, RT], F32, tag="p")
-            nc.vector.scalar_tensor_tensor(out=prod[:], in0=banks[1][:], scalar=bias_t[:, g, 4 + ob:5 + ob],
+            nc.vector.scalar_tensor_tensor(out=prod[:], in0=bank[:], scalar=bias_t[1][:, ob, g:g + 1],
                                            in1=u_sb[:], op0=ALU.add, op1=ALU.mult)
             return prod
 
-        def pool_and_root(ob, rt, prods):
-            z = pz.tile([P, A, P], F32, tag="z")
-            for a in range(A):
-                for g in range(G):
-                    nc.tensor.matmul(out=z[:, a, :], lhsT=prods[g][:, a * P:(a + 1) * P], rhs=ident[:],
-                                     start=(g == 0), stop=(g == G - 1), is_transpose=True)
-            w_sb = wpool.tile([P, A, P], F32, tag="w")
-            nc.scalar.activation(out=w_sb[:], in_=z[:], func=ACT.Abs_reciprocal_sqrt)
-            nc.vector.scalar_tensor_tensor(out=y[:, rt, :, ob * P:(ob + 1) * P], in0=w_sb[:], scalar=BIG,
-                                           in1=z[:], op0=ALU.min, op1=ALU.mult)
+        def add_pair(p0, p1):
+            s = apool.tile([P, RT], F32, tag="s")
+            nc.gpsimd.tensor_tensor(out=s[:], in0=p0[:], in1=p1[:], op=ALU.add)
+            return s
+
+        def pool_terms(z, terms, first, last):
+            for k, term in enumerate(terms):
+                for a in range(A):
+                    nc.tensor.matmul(out=z[:, a, :], lhsT=term[:, a * P:(a + 1) * P], rhs=ident[:],
+                                     start=(first and k == 0 and a == 0),
+                                     stop=(last and k == len(terms) - 1 and a == A - 1), is_transpose=True)
+
+        def root_s(z, a0, a1):
+            w_sb = rpool.tile([P, A, P], F32, tag="w")
+            nc.scalar.activation(out=w_sb[:, a0:a1], in_=z[:, a0:a1], func=ACT.Abs_reciprocal_sqrt)
+            return w_sb
+
+        def root_v(ob, rt, z, w_sb, a0, a1):
+            nc.vector.scalar_tensor_tensor(out=y[rt][:, a0:a1, ob * P:(ob + 1) * P], in0=w_sb[:, a0:a1], scalar=BIG,
+                                           in1=z[:, a0:a1], op0=ALU.min, op1=ALU.mult)
+
+        def squares(rt, k, c0, c1, a0=0, a1=A):
+            for a in range(a0, a1):
+                junk = rpool.tile([P, O], F32, tag="junk")
+                nc.scalar.activation(out=junk[:, 0:c1 - c0], in_=y[rt][:, a, c0:c1], func=ACT.Square,
+                                     accum_out=part[rt][k][:, a:a + 1])
 
         out_v = out.rearrange("(t p a) o -> t p a o", t=N_RT, a=A)
 
         def finish(rt):
-            cols = slice(rt * A, (rt + 1) * A)
+            nc.vector.tensor_tensor(out=ssum[rt][:], in0=part[rt][0][:], in1=part[rt][1][:], op=ALU.add)
+            nc.scalar.activation(out=rn[rt][:], in_=ssum[rt][:], func=ACT.Abs_reciprocal_sqrt)
+            nc.vector.tensor_scalar_min(out=rn[rt][:], in0=rn[rt][:], scalar1=1.0e12)
             for a in range(A):
-                junk = wpool.tile([P, O], F32, tag="junk")
-                nc.scalar.activation(out=junk[:], in_=y[:, rt, a, :], func=ACT.Square,
-                                     accum_out=ssum[:, rt * A + a:rt * A + a + 1])
-            nc.scalar.activation(out=rn_raw[:, cols], in_=ssum[:, cols], func=ACT.Abs_reciprocal_sqrt)
-            nc.vector.tensor_scalar_min(out=rn[:, cols], in0=rn_raw[:, cols], scalar1=1.0e12)
-            last = rt == N_RT - 1
-            for a in range(A):
-                sc = rn[:, rt * A + a:rt * A + a + 1]
-                if last and a < 2:
-                    nc.vector.tensor_scalar_mul(out=y[:, rt, a, :], in0=y[:, rt, a, :], scalar1=sc)
-                elif last and a == 2:
-                    nc.scalar.activation(out=y[:, rt, a, :], in_=y[:, rt, a, :], func=ACT.Copy, scale=sc)
-                else:
-                    nc.gpsimd.tensor_scalar(out=y[:, rt, a, :], in0=y[:, rt, a, :], scalar1=sc, scalar2=0.0,
-                                            op0=ALU.mult, op1=ALU.add)
-                if last:
-                    nc.sync.dma_start(out=out_v[rt][:, a, :], in_=y[:, rt, a, :])
-            if not last:
-                nc.sync.dma_start(out=out_v[rt], in_=y[:, rt])
+                nc.gpsimd.tensor_scalar(out=y[rt][:, a, :], in0=y[rt][:, a, :], scalar1=rn[rt][:, a:a + 1], scalar2=0.0,
+                                        op0=ALU.mult, op1=ALU.add)
+            nc.sync.dma_start(out=out_v[rt], in_=y[rt][:])
 
-        prep_x(0, 0)
-        prep_w(0, 0)
-        prep_x(1, 0)
-        prep_w(1, 0)
-        pending = None
-        for ob in range(N_OB):
-            for rt in range(N_RT):
-                prods = []
+        def finish_last(rt):
+            squares(rt, 2, 3 * P, O)
+            nc.vector.tensor_tensor(out=ssum[rt][:], in0=ssum[rt][:], in1=part[rt][2][:], op=ALU.add)
+            nc.scalar.activation(out=rn[rt][:], in_=ssum[rt][:], func=ACT.Abs_reciprocal_sqrt)
+            nc.vector.tensor_scalar_min(out=rn[rt][:], in0=rn[rt][:], scalar1=1.0e12)
+            for a in range(A):
+                sc = rn[rt][:, a:a + 1]
+                if a == 1:
+                    nc.scalar.activation(out=y[rt][:, a, :], in_=y[rt][:, a, :], func=ACT.Copy, scale=sc)
+                elif a == 3:
+                    nc.gpsimd.tensor_scalar(out=y[rt][:, a, :], in0=y[rt][:, a, :], scalar1=sc, scalar2=0.0,
+                                            op0=ALU.mult, op1=ALU.add)
+                else:
+                    nc.vector.tensor_scalar_mul(out=y[rt][:, a, :], in0=y[rt][:, a, :], scalar1=sc)
+            for a in (0, 2, 1, 3):
+                nc.sync.dma_start(out=out_v[rt][:, a, :], in_=y[rt][:, a, :])
+
+        turn_x(0, 0, "SV")
+        quant_x(0, 0)
+        for g in range(G):
+            regroup_w(0, 0, g, HEAD_ENG[g])
+        for g in range(G):
+            quant_w(0, 0, g, 1)
+        turn_x(1, 0, "SV")
+        quant_x(1, 0)
+        for g in range(G):
+            regroup_w(1, 0, g, HEAD_ENG[g])
+        for g in range(G):
+            quant_w(1, 0, g, 1)
+
+        side = {}
+
+        def at(u, f, *args):
+            side.setdefault(u, []).append((f, args))
+
+        for rt in range(1, N_RT):
+            for x in range(2):
+                at(5 * (rt - 1) + X_AT[x], turn_x, x, rt, X_ENG)
+                at(5 * (rt - 1) + X_AT[x] + X_LAG, quant_x, x, rt)
+        for ob in range(1, N_OB):
+            for w in range(2):
                 for g in range(G):
-                    prods.append(passes(ob, rt, g))
-                    if g == TAIL_AT and pending is not None:
-                        pool_and_root(*pending)
-                        if pending[0] == N_OB - 1:
-                            finish(pending[1])
-                pending = (ob, rt, prods)
-                if ob == 0 and rt + 1 < N_RT:
-                    prep_x(0, rt + 1)
-                    prep_x(1, rt + 1)
-                if rt == 0 and ob + 1 < N_OB:
-                    prep_w(0, ob + 1)
-                    prep_w(1, ob + 1)
-        pool_and_root(*pending)
-        finish(pending[1])
+                    u = 15 * (ob - 1) + W_AT + (w * G + g) * W_STEP // 10
+                    at(u, regroup_w, w, ob, g, BODY_ENG[w][g])
+                    at(u + W_LAG, quant_w, w, ob, g, 1)
+
+        sums = {}
+
+        def tail_t(n, terms):
+            z = pz.tile([P, A, P], F32, tag="z")
+            sums[n] = z
+            pool_terms(z, terms, True, True)
+
+        roots = {}
+
+        def tail_s(n):
+            roots[n] = root_s(sums[n], 0, A)
+
+        def tail_v(n):
+            root_v(n // N_RT, n % N_RT, sums[n], roots[n], 0, A)
+
+        def sum_early(rt):
+            nc.vector.tensor_tensor(out=ssum[rt][:], in0=part[rt][0][:], in1=part[rt][1][:], op=ALU.add)
+
+        for n in range(N_OB * N_RT - 1):
+            p_ob, p_rt = n // N_RT, n % N_RT
+            u = 5 * n + 5
+            at(u + T_AT + S_AT, tail_s, n)
+            at(u + T_AT + S_AT + V_AT, tail_v, n)
+            if p_ob == 1:
+                for a in range(A):
+                    at(u + T_AT + S_AT + V_AT + Q_AT + a * Q_STEP // 2, squares, p_rt, 0, 0, 2 * P, a, a + 1)
+            if p_ob == 2 and p_rt == N_RT - 1:
+                for a in range(A):
+                    at(u + T_AT + S_AT + V_AT + Q_AT + a * Q_STEP // 2, squares, p_rt, 1, 2 * P, 3 * P, a, a + 1)
+                at(u + T_AT + S_AT + V_AT + Q_AT + 3 * Q_STEP // 2, sum_early, p_rt)
+            if p_ob == N_OB - 1:
+                for a in range(A):
+                    at(u + T_AT + S_AT + V_AT + Q_AT + a * Q_STEP // 2, squares, p_rt, 1, 2 * P, O, a, a + 1)
+                at(u + T_AT + S_AT + V_AT + Q_AT + 3 * Q_STEP // 2 + F_AT, finish, p_rt)
+
+        N_U = N_OB * N_RT * G
+        u_tiles = {}
+        prods = {}
+        terms = []
+        for i in range(N_U + VLAG):
+            if i < N_U:
+                n, g = i // G, i % G
+                bank = one_pass(0, n // N_RT, n % N_RT, g)
+                u_tiles[i] = take_u(n // N_RT, g, bank)
+            j = i - VLAG
+            if j >= 0:
+                n, g = j // G, j % G
+                last = n == N_OB * N_RT - 1
+                bank = one_pass(1, n // N_RT, n % N_RT, g)
+                prods[j] = product(n // N_RT, g, bank, u_tiles[j])
+                if g == 0:
+                    terms = []
+                if not last and (g == 1 or (g == 3 and ADDS == 2)):
+                    terms.append(add_pair(prods[j - 1], prods[j]))
+                elif last or g == 4 or ADDS == 0 or (g >= 2 and ADDS < 2):
+                    terms.append(prods[j])
+                for f, args in side.get(j, ()):
+                    f(*args)
+                if g == G - 1:
+                    at(j + 1 + T_AT, tail_t, n, terms)
+                    side[j + 1 + T_AT] = side[j + 1 + T_AT][-1:] + side[j + 1 + T_AT][:-1]
+        for u in range(5 * N_OB * N_RT, 5 * N_OB * N_RT + 12):
+            for f, args in side.get(u, ()):
+                if f != tail_t:
+                    f(*args)
+        z = pz.tile([P, A, P], F32, tag="z")
+        pool_terms(z, terms, True, True)
+        w_sb = root_s(z, 0, A)
+        root_v(N_OB - 1, N_RT - 1, z, w_sb, 0, A)
+        finish_last(N_RT - 1)

@@ -24,22 +24,27 @@ BIG = 1.0e19
 PU = 3
 PV = 3
 PZ = 2
-VLAG = 2
-T_AT = 0
-S_AT = 0
+VLAG = 1
+ADDS = (0, 0, 1, 1, 1, 1, 1, 1, 1, 2, 2, 1)
+T_AT = 3
+S_AT = 2
 V_AT = 1
 Q_AT = 2
-Q_STEP = 0
-F_AT = 1
-HEAD_ENG = "VVSSS"
-BODY_ENG = ("GGGGV", "GGGGG")
-ADDS = 1
-X_AT = (0, 1)
-X_LAG = 1
-X_ENG = "SS"
-W_AT = 1
-W_STEP = 13
-W_LAG = 3
+Q_STEP = 3
+N_AT = 2
+F_AT = 0
+F_STEP = 1
+FIN = ('GGVV', 'SVSV', 'VVSS')
+SQ = ((2, 0, 3, 'SSVV'),)
+W_Q = ((0, 4), (4, 1))
+Q_U = 1
+P_U = 3
+P_ENG = 'GGGGSGGGGS'
+PIECES = (5, 5, 4, 3, 3, 4, 3, 3, 0, 0, 0, 0)
+X_T = (0, 1, 3, 4)
+X_Q = (1, 2, 4, 5)
+X_ENG = ('SS', 'SS', 'SV', 'SS')
+HEAD_ENG = ("VVVSS", "VVSSS")
 
 
 def tile_gnn_new_pb_kernel(tc, h, neighbours, W_node, b_node, W_nb, b_nb, out):
@@ -50,8 +55,8 @@ def tile_gnn_new_pb_kernel(tc, h, neighbours, W_node, b_node, W_nb, b_nb, out):
         keep = ctx.enter_context(tc.tile_pool(name="keep", bufs=1))
         xstage = ctx.enter_context(tc.tile_pool(name="xstage", bufs=3))
         wstage = ctx.enter_context(tc.tile_pool(name="wstage", bufs=4))
-        upool = ctx.enter_context(tc.tile_pool(name="upool", bufs=6))
-        ppool = ctx.enter_context(tc.tile_pool(name="ppool", bufs=12))
+        upool = ctx.enter_context(tc.tile_pool(name="upool", bufs=4 + VLAG))
+        ppool = ctx.enter_context(tc.tile_pool(name="ppool", bufs=16))
         apool = ctx.enter_context(tc.tile_pool(name="apool", bufs=4))
         rpool = ctx.enter_context(tc.tile_pool(name="rpool", bufs=2))
         pu = ctx.enter_context(tc.psum_pool(name="pu", bufs=PU))
@@ -69,7 +74,7 @@ def tile_gnn_new_pb_kernel(tc, h, neighbours, W_node, b_node, W_nb, b_nb, out):
         bias_t = [keep.tile([P, N_OB, 6], BF16, name="bias%d" % w) for w in range(2)]
         one = keep.tile([P, 1], F32, name="one")
         warm = keep.tile([P, 1], F32, name="warm")
-        part = [[keep.tile([P, A], F32, name="part%d%d" % (rt, k)) for k in range(3)] for rt in range(N_RT)]
+        part = [[keep.tile([P, A], F32, name="part%d%d" % (rt, k)) for k in range(len(SQ) + 1)] for rt in range(N_RT)]
         ssum = [keep.tile([P, A], F32, name="ssum%d" % rt) for rt in range(N_RT)]
         rn = [keep.tile([P, A], F32, name="rn%d" % rt) for rt in range(N_RT)]
 
@@ -89,10 +94,9 @@ def tile_gnn_new_pb_kernel(tc, h, neighbours, W_node, b_node, W_nb, b_nb, out):
                 )
 
         nc.vector.memset(one[:], 1.0)
-        load_x(0, 0)
-        load_w(0, 0)
-        load_x(1, 0)
-        load_w(1, 0)
+        for k in range(2):
+            load_x(k, 0)
+            load_w(k, 0)
         for w, b in enumerate((b_node, b_nb)):
             nc.sync.dma_start(out=bias_t[w][:, :, 0:G], in_=b.rearrange("(o m g) -> m o g", o=N_OB, g=G))
         for rt in range(1, N_RT):
@@ -188,114 +192,121 @@ def tile_gnn_new_pb_kernel(tc, h, neighbours, W_node, b_node, W_nb, b_nb, out):
                                      start=(first and k == 0 and a == 0),
                                      stop=(last and k == len(terms) - 1 and a == A - 1), is_transpose=True)
 
-        def root_s(z, a0, a1):
-            w_sb = rpool.tile([P, A, P], F32, tag="w")
-            nc.scalar.activation(out=w_sb[:, a0:a1], in_=z[:, a0:a1], func=ACT.Abs_reciprocal_sqrt)
-            return w_sb
-
-        def root_v(ob, rt, z, w_sb, a0, a1):
-            nc.vector.scalar_tensor_tensor(out=y[rt][:, a0:a1, ob * P:(ob + 1) * P], in0=w_sb[:, a0:a1], scalar=BIG,
-                                           in1=z[:, a0:a1], op0=ALU.min, op1=ALU.mult)
-
-        def squares(rt, k, c0, c1, a0=0, a1=A):
-            for a in range(a0, a1):
-                junk = rpool.tile([P, O], F32, tag="junk")
-                nc.scalar.activation(out=junk[:, 0:c1 - c0], in_=y[rt][:, a, c0:c1], func=ACT.Square,
-                                     accum_out=part[rt][k][:, a:a + 1])
-
-        out_v = out.rearrange("(t p a) o -> t p a o", t=N_RT, a=A)
-
-        def finish(rt):
-            nc.vector.tensor_tensor(out=ssum[rt][:], in0=part[rt][0][:], in1=part[rt][1][:], op=ALU.add)
-            nc.scalar.activation(out=rn[rt][:], in_=ssum[rt][:], func=ACT.Abs_reciprocal_sqrt)
-            nc.vector.tensor_scalar_min(out=rn[rt][:], in0=rn[rt][:], scalar1=1.0e12)
-            for a in range(A):
-                nc.gpsimd.tensor_scalar(out=y[rt][:, a, :], in0=y[rt][:, a, :], scalar1=rn[rt][:, a:a + 1], scalar2=0.0,
-                                        op0=ALU.mult, op1=ALU.add)
-            nc.sync.dma_start(out=out_v[rt], in_=y[rt][:])
-
-        def finish_last(rt):
-            squares(rt, 2, 3 * P, O)
-            nc.vector.tensor_tensor(out=ssum[rt][:], in0=ssum[rt][:], in1=part[rt][2][:], op=ALU.add)
-            nc.scalar.activation(out=rn[rt][:], in_=ssum[rt][:], func=ACT.Abs_reciprocal_sqrt)
-            nc.vector.tensor_scalar_min(out=rn[rt][:], in0=rn[rt][:], scalar1=1.0e12)
-            for a in range(A):
-                sc = rn[rt][:, a:a + 1]
-                if a == 1:
-                    nc.scalar.activation(out=y[rt][:, a, :], in_=y[rt][:, a, :], func=ACT.Copy, scale=sc)
-                elif a == 3:
-                    nc.gpsimd.tensor_scalar(out=y[rt][:, a, :], in0=y[rt][:, a, :], scalar1=sc, scalar2=0.0,
-                                            op0=ALU.mult, op1=ALU.add)
-                else:
-                    nc.vector.tensor_scalar_mul(out=y[rt][:, a, :], in0=y[rt][:, a, :], scalar1=sc)
-            for a in (0, 2, 1, 3):
-                nc.sync.dma_start(out=out_v[rt][:, a, :], in_=y[rt][:, a, :])
-
-        turn_x(0, 0, "SV")
-        quant_x(0, 0)
-        for g in range(G):
-            regroup_w(0, 0, g, HEAD_ENG[g])
-        for g in range(G):
-            quant_w(0, 0, g, 1)
-        turn_x(1, 0, "SV")
-        quant_x(1, 0)
-        for g in range(G):
-            regroup_w(1, 0, g, HEAD_ENG[g])
-        for g in range(G):
-            quant_w(1, 0, g, 1)
-
+        N_G = N_OB * N_RT
+        N_U = N_G * G
         side = {}
 
         def at(u, f, *args):
             side.setdefault(u, []).append((f, args))
 
-        for rt in range(1, N_RT):
-            for x in range(2):
-                at(5 * (rt - 1) + X_AT[x], turn_x, x, rt, X_ENG)
-                at(5 * (rt - 1) + X_AT[x] + X_LAG, quant_x, x, rt)
-        for ob in range(1, N_OB):
-            for w in range(2):
-                for g in range(G):
-                    u = 15 * (ob - 1) + W_AT + (w * G + g) * W_STEP // 10
-                    at(u, regroup_w, w, ob, g, BODY_ENG[w][g])
-                    at(u + W_LAG, quant_w, w, ob, g, 1)
-
         sums = {}
+        roots = {}
 
         def tail_t(n, terms):
             z = pz.tile([P, A, P], F32, tag="z")
             sums[n] = z
             pool_terms(z, terms, True, True)
 
-        roots = {}
-
         def tail_s(n):
-            roots[n] = root_s(sums[n], 0, A)
+            w_sb = rpool.tile([P, A, P], F32, tag="w")
+            roots[n] = w_sb
+            nc.scalar.activation(out=w_sb[:], in_=sums[n][:], func=ACT.Abs_reciprocal_sqrt)
 
         def tail_v(n):
-            root_v(n // N_RT, n % N_RT, sums[n], roots[n], 0, A)
+            ob, rt = n // N_RT, n % N_RT
+            nc.vector.scalar_tensor_tensor(out=y[rt][:, :, ob * P:(ob + 1) * P], in0=roots[n][:], scalar=BIG,
+                                           in1=sums[n][:], op0=ALU.min, op1=ALU.mult)
+
+        def squares(rt, k, c0, c1, a, eng):
+            src = y[rt][:, a, c0:c1]
+            acc = part[rt][k][:, a:a + 1]
+            if eng == "S":
+                junk = rpool.tile([P, O], F32, tag="junk")
+                nc.scalar.activation(out=junk[:, 0:c1 - c0], in_=src, func=ACT.Square, accum_out=acc)
+            else:
+                junk_v = rpool.tile([P, O], F32, tag="junk_v")
+                nc.vector.scalar_tensor_tensor(out=junk_v[:, 0:c1 - c0], in0=src, scalar=1.0, in1=src,
+                                               op0=ALU.mult, op1=ALU.mult, accum_out=acc)
 
         def sum_early(rt):
-            nc.vector.tensor_tensor(out=ssum[rt][:], in0=part[rt][0][:], in1=part[rt][1][:], op=ALU.add)
+            total = part[rt][0]
+            if len(SQ) > 1:
+                total = ssum[rt]
+                nc.vector.tensor_tensor(out=total[:], in0=part[rt][0][:], in1=part[rt][1][:], op=ALU.add)
+            nc.vector.tensor_scalar_max(out=ssum[rt][:], in0=total[:], scalar1=1.0e-24)
 
-        for n in range(N_OB * N_RT - 1):
-            p_ob, p_rt = n // N_RT, n % N_RT
-            u = 5 * n + 5
-            at(u + T_AT + S_AT, tail_s, n)
-            at(u + T_AT + S_AT + V_AT, tail_v, n)
-            if p_ob == 1:
-                for a in range(A):
-                    at(u + T_AT + S_AT + V_AT + Q_AT + a * Q_STEP // 2, squares, p_rt, 0, 0, 2 * P, a, a + 1)
-            if p_ob == 2 and p_rt == N_RT - 1:
-                for a in range(A):
-                    at(u + T_AT + S_AT + V_AT + Q_AT + a * Q_STEP // 2, squares, p_rt, 1, 2 * P, 3 * P, a, a + 1)
-                at(u + T_AT + S_AT + V_AT + Q_AT + 3 * Q_STEP // 2, sum_early, p_rt)
-            if p_ob == N_OB - 1:
-                for a in range(A):
-                    at(u + T_AT + S_AT + V_AT + Q_AT + a * Q_STEP // 2, squares, p_rt, 1, 2 * P, O, a, a + 1)
-                at(u + T_AT + S_AT + V_AT + Q_AT + 3 * Q_STEP // 2 + F_AT, finish, p_rt)
+        def norm(n):
+            rt = n % N_RT
+            for a in range(A):
+                junk = rpool.tile([P, O], F32, tag="junk")
+                nc.scalar.activation(out=junk[:, 0:P], in_=sums[n][:, a, :], func=ACT.Abs,
+                                     accum_out=part[rt][len(SQ)][:, a:a + 1])
+            for a in range(A):
+                nc.scalar.activation(out=rn[rt][:, a:a + 1], in_=part[rt][len(SQ)][:, a:a + 1],
+                                     func=ACT.Abs_reciprocal_sqrt, bias=ssum[rt][:, a:a + 1])
 
-        N_U = N_OB * N_RT * G
+        out_v = out.rearrange("(t p a) o -> t p a o", t=N_RT, a=A)
+
+        def scale(rt, a, eng):
+            sc = rn[rt][:, a:a + 1]
+            t = y[rt][:, a, :]
+            if eng == "S":
+                nc.scalar.activation(out=t, in_=t, func=ACT.Copy, scale=sc)
+            elif eng == "G":
+                nc.gpsimd.tensor_scalar(out=t, in0=t, scalar1=sc, scalar2=0.0, op0=ALU.mult, op1=ALU.add)
+            else:
+                nc.vector.tensor_scalar_mul(out=t, in0=t, scalar1=sc)
+
+        def store(rt, a0, a1):
+            nc.sync.dma_start(out=out_v[rt][:, a0:a1], in_=y[rt][:, a0:a1, :])
+
+        turn_x(0, 0, "VS")
+        for g in range(G):
+            regroup_w(0, 0, g, HEAD_ENG[0][g])
+        quant_x(0, 0)
+        quant_w(0, 0, 0, 1)
+        turn_x(1, 0, "VS")
+        quant_w(0, 0, 1, 4)
+        for g in range(G):
+            regroup_w(1, 0, g, HEAD_ENG[1][g])
+        quant_x(1, 0)
+        quant_w(1, 0, 0, 1)
+        quant_w(1, 0, 1, 4)
+
+        for i in range(4):
+            rt, x = 1 + i // 2, i % 2
+            at(X_T[i], turn_x, x, rt, X_ENG[i])
+            at(X_Q[i], quant_x, x, rt)
+        q = 0
+        done = []
+        for n in range(N_G):
+            for w, ob in done:
+                for g0, k in W_Q:
+                    at(5 * n + Q_U, quant_w, w, ob, g0, k)
+            done = []
+            for c in range(PIECES[n]):
+                ob, w, g = 1 + q // 10, q % 10 // G, q % G
+                at(5 * n + P_U, regroup_w, w, ob, g, P_ENG[q % 10])
+                if g == G - 1:
+                    done.append((w, ob))
+                q += 1
+        for n in range(N_G - 1):
+            ob, rt = n // N_RT, n % N_RT
+            u = 5 * n + 5 + T_AT
+            at(u + S_AT, tail_s, n)
+            at(u + S_AT + V_AT, tail_v, n)
+            for k, (b, c0, c1, engs) in enumerate(SQ):
+                if b == ob:
+                    for a in range(A):
+                        at(u + S_AT + V_AT + Q_AT + a * Q_STEP // 2, squares, rt, k, c0 * P, c1 * P, a, engs[a])
+                    if k == len(SQ) - 1:
+                        at(u + S_AT + V_AT + Q_AT + 3 * Q_STEP // 2 + 1, sum_early, rt)
+            if ob == N_OB - 1:
+                at(u + S_AT + N_AT, norm, n)
+                for a in range(A):
+                    at(u + S_AT + max(N_AT, V_AT) + F_AT + a * F_STEP // 2, scale, rt, a, FIN[rt][a])
+                at(u + S_AT + max(N_AT, V_AT) + F_AT + 3 * F_STEP // 2, store, rt, 0, A)
+
         u_tiles = {}
         prods = {}
         terms = []
@@ -307,26 +318,31 @@ def tile_gnn_new_pb_kernel(tc, h, neighbours, W_node, b_node, W_nb, b_nb, out):
             j = i - VLAG
             if j >= 0:
                 n, g = j // G, j % G
-                last = n == N_OB * N_RT - 1
                 bank = one_pass(1, n // N_RT, n % N_RT, g)
                 prods[j] = product(n // N_RT, g, bank, u_tiles[j])
                 if g == 0:
                     terms = []
-                if not last and (g == 1 or (g == 3 and ADDS == 2)):
+                if (g == 1 and ADDS[n] > 0) or (g == 3 and ADDS[n] > 1):
                     terms.append(add_pair(prods[j - 1], prods[j]))
-                elif last or g == 4 or ADDS == 0 or (g >= 2 and ADDS < 2):
+                elif g == 4 or (g >= 2 and ADDS[n] < 2) or ADDS[n] == 0:
                     terms.append(prods[j])
-                for f, args in side.get(j, ()):
-                    f(*args)
-                if g == G - 1:
+                first = side.get(j, [])
+                for f, args in first:
+                    if f == tail_t:
+                        f(*args)
+                for f, args in first:
+                    if f != tail_t:
+                        f(*args)
+                if g == G - 1 and n < N_G - 1:
                     at(j + 1 + T_AT, tail_t, n, terms)
-                    side[j + 1 + T_AT] = side[j + 1 + T_AT][-1:] + side[j + 1 + T_AT][:-1]
-        for u in range(5 * N_OB * N_RT, 5 * N_OB * N_RT + 12):
+        n = N_G - 1
+        tail_t(n, terms)
+        for u in range(N_U, N_U + 12):
             for f, args in side.get(u, ()):
-                if f != tail_t:
-                    f(*args)
-        z = pz.tile([P, A, P], F32, tag="z")
-        pool_terms(z, terms, True, True)
-        w_sb = root_s(z, 0, A)
-        root_v(N_OB - 1, N_RT - 1, z, w_sb, 0, A)
-        finish_last(N_RT - 1)
+                f(*args)
+        tail_s(n)
+        norm(n)
+        tail_v(n)
+        for a in range(A):
+            scale(N_RT - 1, a, FIN[N_RT - 1][a])
+            store(N_RT - 1, a, a + 1)

@@ -71,7 +71,9 @@ def tile_gnn_new_pb_kernel(tc, h, neighbours, W_node, b_node, W_nb, b_nb, out):
         ws = [[keep.tile([P, CH], U8, name="ws%d%d" % (w, ob), align_bytes=64) for ob in range(N_OB)] for w in range(2)]
         y = [keep.tile([P, A, O], F32, name="y%d" % rt) for rt in range(N_RT)]
         ident = keep.tile([P, P], F32, name="ident")
-        bias_t = [keep.tile([P, N_OB, 6], BF16, name="bias%d" % w) for w in range(2)]
+        ident_b = keep.tile([P, P], BF16, name="ident_b")
+        braw = keep.tile([P, CH], BF16, name="braw")
+        bias_t = keep.tile([P, G, 2 * N_OB], F32, name="bias_t")
         one = keep.tile([P, 1], F32, name="one")
         warm = keep.tile([P, 1], F32, name="warm")
         part = [[keep.tile([P, A], F32, name="part%d%d" % (rt, k)) for k in range(len(SQ) + 1)] for rt in range(N_RT)]
@@ -93,12 +95,14 @@ def tile_gnn_new_pb_kernel(tc, h, neighbours, W_node, b_node, W_nb, b_nb, out):
                     in_=weights[w][256 * u:256 * u + 256, ob * CH:(ob + 1) * CH].rearrange("(q e) c -> q e c", e=2),
                 )
 
+        nc.gpsimd.memset(braw[:].bitcast(F32), 0.0)
         nc.vector.memset(one[:], 1.0)
-        for k in range(2):
-            load_x(k, 0)
-            load_w(k, 0)
-        for w, b in enumerate((b_node, b_nb)):
-            nc.sync.dma_start(out=bias_t[w][:, :, 0:G], in_=b.rearrange("(o m g) -> m o g", o=N_OB, g=G))
+        load_x(0, 0)
+        nc.sync.dma_start(out=braw[0:N_OB, :], in_=b_node.rearrange("(o c) -> o c", o=N_OB))
+        nc.sync.dma_start(out=braw[N_OB:2 * N_OB, :], in_=b_nb.rearrange("(o c) -> o c", o=N_OB))
+        load_w(0, 0)
+        load_x(1, 0)
+        load_w(1, 0)
         for rt in range(1, N_RT):
             load_x(0, rt)
             load_x(1, rt)
@@ -106,7 +110,15 @@ def tile_gnn_new_pb_kernel(tc, h, neighbours, W_node, b_node, W_nb, b_nb, out):
             load_w(0, ob)
             load_w(1, ob)
         make_identity(nc, ident[:])
+        make_identity(nc, ident_b[:])
         nc.scalar.activation(out=warm[:], in_=one[:], func=ACT.Abs_reciprocal_sqrt)
+
+        def turn_bias():
+            cols = braw[:].rearrange("p (m g) -> p g m", g=G)
+            t = pz.tile([P, G, P], BF16, tag="z")
+            for g in range(G):
+                nc.tensor.transpose(t[:, g, :], cols[:, g, :], ident_b[:])
+            nc.vector.tensor_copy(out=bias_t[:], in_=t[:, :, 0:2 * N_OB])
 
         xg = {}
 
@@ -171,12 +183,12 @@ def tile_gnn_new_pb_kernel(tc, h, neighbours, W_node, b_node, W_nb, b_nb, out):
         def take_u(ob, g, bank):
             u_sb = upool.tile([P, RT], F32, tag="usb")
             nc.scalar.activation(out=u_sb[:], in_=bank[:], func=ACT.Identity,
-                                 bias=bias_t[0][:, ob, g:g + 1], scale=1.0)
+                                 bias=bias_t[:, g, ob:ob + 1], scale=1.0)
             return u_sb
 
         def product(ob, g, bank, u_sb):
             prod = ppool.tile([P, RT], F32, tag="p")
-            nc.vector.scalar_tensor_tensor(out=prod[:], in0=bank[:], scalar=bias_t[1][:, ob, g:g + 1],
+            nc.vector.scalar_tensor_tensor(out=prod[:], in0=bank[:], scalar=bias_t[:, g, N_OB + ob:N_OB + ob + 1],
                                            in1=u_sb[:], op0=ALU.add, op1=ALU.mult)
             return prod
 
@@ -261,6 +273,7 @@ def tile_gnn_new_pb_kernel(tc, h, neighbours, W_node, b_node, W_nb, b_nb, out):
             nc.sync.dma_start(out=out_v[rt][:, a0:a1], in_=y[rt][:, a0:a1, :])
 
         turn_x(0, 0, "VS")
+        turn_bias()
         for g in range(G):
             regroup_w(0, 0, g, HEAD_ENG[0][g])
         quant_x(0, 0)

@@ -25,25 +25,25 @@ PU = 3
 PV = 3
 PZ = 2
 VLAG = 1
-ADDS = (0, 0, 1, 1, 1, 1, 1, 1, 1, 2, 2, 1)
+ADDS = (0, 0, 1, 1, 1, 1, 1, 1, 1, 2, 2, 0)
 T_AT = 3
 S_AT = 2
 V_AT = 1
 Q_AT = 2
 Q_STEP = 3
 N_AT = 2
-F_AT = 0
-F_STEP = 1
-FIN = ('GGVV', 'SVSV', 'VVSS')
+F_AT = 1
+F_STEP = 2
+FIN = ('GGVV', 'VVVV', 'VVSV')
 SQ = ((2, 0, 3, 'SSVV'),)
-W_Q = ((0, 4), (4, 1))
-Q_U = 1
-P_U = 3
+W_Q = ((0, 8), (8, 2))
+Q_U = 0
+P_U = 1
 P_ENG = 'GGGGSGGGGS'
 PIECES = (5, 5, 4, 3, 3, 4, 3, 3, 0, 0, 0, 0)
-X_T = (0, 1, 3, 4)
-X_Q = (1, 2, 4, 5)
-X_ENG = ('SS', 'SS', 'SV', 'SS')
+X_T = (0, 1, 2, 3)
+X_Q = (1, 6)
+X_ENG = ('SV', 'SV', 'SV', 'SV')
 HEAD_ENG = ("VVVSS", "VVSSS")
 
 
@@ -53,10 +53,10 @@ def tile_gnn_new_pb_kernel(tc, h, neighbours, W_node, b_node, W_nb, b_nb, out):
     weights = (W_node, W_nb)
     with ExitStack() as ctx:
         keep = ctx.enter_context(tc.tile_pool(name="keep", bufs=1))
-        xstage = ctx.enter_context(tc.tile_pool(name="xstage", bufs=3))
-        wstage = ctx.enter_context(tc.tile_pool(name="wstage", bufs=4))
+        xstage = ctx.enter_context(tc.tile_pool(name="xstage", bufs=2))
+        wstage = ctx.enter_context(tc.tile_pool(name="wstage", bufs=2))
         upool = ctx.enter_context(tc.tile_pool(name="upool", bufs=4 + VLAG))
-        ppool = ctx.enter_context(tc.tile_pool(name="ppool", bufs=16))
+        ppool = ctx.enter_context(tc.tile_pool(name="ppool", bufs=12))
         apool = ctx.enter_context(tc.tile_pool(name="apool", bufs=4))
         rpool = ctx.enter_context(tc.tile_pool(name="rpool", bufs=2))
         pu = ctx.enter_context(tc.psum_pool(name="pu", bufs=PU))
@@ -65,10 +65,10 @@ def tile_gnn_new_pb_kernel(tc, h, neighbours, W_node, b_node, W_nb, b_nb, out):
 
         xraw = [[keep.tile([P, A * D], BF16, name="xraw%d%d" % (x, rt)) for rt in range(N_RT)] for x in range(2)]
         wraw = [[keep.tile([P, 4, CH], BF16, name="wraw%d%d" % (w, ob)) for ob in range(N_OB)] for w in range(2)]
-        xc = [[keep.tile([P, RT], U32, name="xc%d%d" % (x, rt), align_bytes=64) for rt in range(N_RT)] for x in range(2)]
-        xs = [[keep.tile([P, RT], U8, name="xs%d%d" % (x, rt), align_bytes=64) for rt in range(N_RT)] for x in range(2)]
-        wc = [[keep.tile([P, CH], U32, name="wc%d%d" % (w, ob), align_bytes=64) for ob in range(N_OB)] for w in range(2)]
-        ws = [[keep.tile([P, CH], U8, name="ws%d%d" % (w, ob), align_bytes=64) for ob in range(N_OB)] for w in range(2)]
+        xc = [keep.tile([P, 2, RT], U32, name="xc%d" % rt, align_bytes=64) for rt in range(N_RT)]
+        xs = [keep.tile([P, 2, RT], U8, name="xs%d" % rt, align_bytes=64) for rt in range(N_RT)]
+        wc = [keep.tile([P, 2, CH], U32, name="wc%d" % ob, align_bytes=64) for ob in range(N_OB)]
+        ws = [keep.tile([P, 2, CH], U8, name="ws%d" % ob, align_bytes=64) for ob in range(N_OB)]
         y = [keep.tile([P, A, O], F32, name="y%d" % rt) for rt in range(N_RT)]
         ident = keep.tile([P, P], F32, name="ident")
         ident_b = keep.tile([P, P], BF16, name="ident_b")
@@ -123,9 +123,10 @@ def tile_gnn_new_pb_kernel(tc, h, neighbours, W_node, b_node, W_nb, b_nb, out):
         xg = {}
 
         def turn_x(x, rt, engines):
-            grouped = xstage.tile([P, 4 * RT], BF16, tag="xg", align_bytes=64)
-            xg[x, rt] = grouped
-            g32 = grouped[:].bitcast(F32).rearrange("q (a c u) -> q a c u", a=A, u=2)
+            if x == 0:
+                grouped = xstage.tile([P, 2, 4 * RT], BF16, tag="xg", align_bytes=64)
+                xg[rt] = grouped
+            g32 = xg[rt][:, x, :].bitcast(F32).rearrange("q (a c u) -> q a c u", a=A, u=2)
             r32 = xraw[x][rt][:].bitcast(F32)
             for half in range(2):
                 t = pz.tile([P, 512], F32, tag="z")
@@ -139,16 +140,20 @@ def tile_gnn_new_pb_kernel(tc, h, neighbours, W_node, b_node, W_nb, b_nb, out):
                 else:
                     nc.vector.tensor_copy(out=dst, in_=src)
 
-        def quant_x(x, rt):
-            nc.vector.quantize_mx(out=xc[x][rt][:].bitcast(FP8X4), scales=xs[x][rt][:], in_=xg[x, rt][:])
+        def quant_x(x, k, rt):
+            nc.vector.quantize_mx(
+                out=xc[rt][:, x:x + k, :].rearrange("p x r -> p (x r)").bitcast(FP8X4),
+                scales=xs[rt][:, x:x + k, :].rearrange("p x r -> p (x r)"),
+                in_=xg[rt][:, x:x + k, :].rearrange("p x r -> p (x r)"),
+            )
 
         wg = {}
 
         def regroup_w(w, ob, g, engine):
-            if g == 0:
-                grouped = wstage.tile([P, G, P, 4], BF16, tag="wg", align_bytes=64)
-                wg[w, ob] = grouped
-            dst = wg[w, ob][:, g]
+            if w == 0 and g == 0:
+                grouped = wstage.tile([P, 2 * G, P, 4], BF16, tag="wg", align_bytes=64)
+                wg[ob] = grouped
+            dst = wg[ob][:, w * G + g]
             src = wraw[w][ob][:].rearrange("q t (m g) -> q g m t", g=G)[:, g]
             if engine == "S":
                 nc.scalar.copy(out=dst, in_=src)
@@ -157,12 +162,12 @@ def tile_gnn_new_pb_kernel(tc, h, neighbours, W_node, b_node, W_nb, b_nb, out):
             else:
                 nc.gpsimd.tensor_scalar(out=dst, in0=src, scalar1=1.0, scalar2=0.0, op0=ALU.mult, op1=ALU.add)
 
-        def quant_w(w, ob, g0, n):
-            cols = slice(g0 * P, (g0 + n) * P)
+        def quant_w(ob, i0, k):
+            cols = slice(i0 * P, (i0 + k) * P)
             nc.vector.quantize_mx(
-                out=wc[w][ob][:, cols].bitcast(FP8X4),
-                scales=ws[w][ob][:, cols],
-                in_=wg[w, ob][:, g0:g0 + n].rearrange("q g m t -> q (g m t)"),
+                out=wc[ob][:].rearrange("p w c -> p (w c)")[:, cols].bitcast(FP8X4),
+                scales=ws[ob][:].rearrange("p w c -> p (w c)")[:, cols],
+                in_=wg[ob][:, i0:i0 + k].rearrange("q i m t -> q (i m t)"),
             )
 
         def one_pass(w, ob, rt, g):
@@ -171,10 +176,10 @@ def tile_gnn_new_pb_kernel(tc, h, neighbours, W_node, b_node, W_nb, b_nb, out):
             bank = pool.tile([P, RT], F32, tag="u" if w == 0 else "v")
             nc.tensor.matmul_mx(
                 out=bank[:],
-                lhsT=wc[w][ob][:, cols].bitcast(FP8X4),
-                lhsT_scale=ws[w][ob][:, cols],
-                rhs=xc[w][rt][:].bitcast(FP8X4),
-                rhs_scale=xs[w][rt][:],
+                lhsT=wc[ob][:, w, cols].bitcast(FP8X4),
+                lhsT_scale=ws[ob][:, w, cols],
+                rhs=xc[rt][:, w, :].bitcast(FP8X4),
+                rhs_scale=xs[rt][:, w, :],
                 start=True,
                 stop=True,
             )
@@ -276,32 +281,33 @@ def tile_gnn_new_pb_kernel(tc, h, neighbours, W_node, b_node, W_nb, b_nb, out):
         turn_bias()
         for g in range(G):
             regroup_w(0, 0, g, HEAD_ENG[0][g])
-        quant_x(0, 0)
-        quant_w(0, 0, 0, 1)
+        quant_x(0, 1, 0)
+        quant_w(0, 0, 1)
         turn_x(1, 0, "VS")
-        quant_w(0, 0, 1, 4)
+        quant_w(0, 1, 4)
         for g in range(G):
             regroup_w(1, 0, g, HEAD_ENG[1][g])
-        quant_x(1, 0)
-        quant_w(1, 0, 0, 1)
-        quant_w(1, 0, 1, 4)
+        quant_x(1, 1, 0)
+        quant_w(0, 5, 1)
+        quant_w(0, 6, 4)
 
         for i in range(4):
             rt, x = 1 + i // 2, i % 2
             at(X_T[i], turn_x, x, rt, X_ENG[i])
-            at(X_Q[i], quant_x, x, rt)
+            if x == 1:
+                at(X_Q[rt - 1], quant_x, 0, 2, rt)
         q = 0
         done = []
         for n in range(N_G):
-            for w, ob in done:
-                for g0, k in W_Q:
-                    at(5 * n + Q_U, quant_w, w, ob, g0, k)
+            for ob in done:
+                for i0, k in W_Q:
+                    at(5 * n + Q_U, quant_w, ob, i0, k)
             done = []
             for c in range(PIECES[n]):
                 ob, w, g = 1 + q // 10, q % 10 // G, q % G
                 at(5 * n + P_U, regroup_w, w, ob, g, P_ENG[q % 10])
-                if g == G - 1:
-                    done.append((w, ob))
+                if q % 10 == 9:
+                    done.append(ob)
                 q += 1
         for n in range(N_G - 1):
             ob, rt = n // N_RT, n % N_RT

@@ -21,13 +21,16 @@ A = RT // P
 CH = P * G
 FLOPS = 2 * 2 * R * D * J
 BIG = 1.0e19
+LATER = (("x", 1), ("w", 1), ("x", 2), ("w", 2), ("w", 3))
 PU = 3
 PV = 3
 PZ = 2
 VLAG = 1
-ADDS = (0, 0, 1, 1, 1, 1, 1, 1, 1, 2, 2, 0)
+ADDS = (1, 0, 1, 1, 1, 1, 1, 1, 1, 2, 2, 0)
+T_LATE = (3, 3)
 T_AT = 3
 S_AT = 2
+S_LATE = (2, 2)
 V_AT = 1
 Q_AT = 2
 Q_STEP = 3
@@ -35,6 +38,7 @@ N_AT = 2
 F_AT = 1
 F_STEP = 2
 FIN = ('GGVV', 'VVVV', 'VVSV')
+STORE = (1, 1)
 SQ = ((2, 0, 3, 'SSVV'),)
 W_Q = ((0, 8), (8, 2))
 Q_U = 0
@@ -44,7 +48,7 @@ PIECES = (5, 5, 4, 3, 3, 4, 3, 3, 0, 0, 0, 0)
 X_T = (0, 1, 2, 3)
 X_Q = (1, 6)
 X_ENG = ('SV', 'SV', 'SV', 'SV')
-HEAD_ENG = ("VVVSS", "VVSSS")
+HEAD_ENG = ("VVSSS", "VVSSS")
 
 
 def tile_gnn_new_pb_kernel(tc, h, neighbours, W_node, b_node, W_nb, b_nb, out):
@@ -103,12 +107,12 @@ def tile_gnn_new_pb_kernel(tc, h, neighbours, W_node, b_node, W_nb, b_nb, out):
         load_w(0, 0)
         load_x(1, 0)
         load_w(1, 0)
-        for rt in range(1, N_RT):
-            load_x(0, rt)
-            load_x(1, rt)
-        for ob in range(1, N_OB):
-            load_w(0, ob)
-            load_w(1, ob)
+        for kind, k in LATER:
+            for i in range(2):
+                if kind == "x":
+                    load_x(i, k)
+                else:
+                    load_w(i, k)
         make_identity(nc, ident[:])
         make_identity(nc, ident_b[:])
         nc.scalar.activation(out=warm[:], in_=one[:], func=ACT.Abs_reciprocal_sqrt)
@@ -216,6 +220,9 @@ def tile_gnn_new_pb_kernel(tc, h, neighbours, W_node, b_node, W_nb, b_nb, out):
         def at(u, f, *args):
             side.setdefault(u, []).append((f, args))
 
+        def t_at(n):
+            return T_AT if n < N_G - 3 else T_LATE[n - (N_G - 3)]
+
         sums = {}
         roots = {}
 
@@ -311,20 +318,22 @@ def tile_gnn_new_pb_kernel(tc, h, neighbours, W_node, b_node, W_nb, b_nb, out):
                 q += 1
         for n in range(N_G - 1):
             ob, rt = n // N_RT, n % N_RT
-            u = 5 * n + 5 + T_AT
-            at(u + S_AT, tail_s, n)
-            at(u + S_AT + V_AT, tail_v, n)
+            u = 5 * n + 5 + t_at(n)
+            s_at = S_AT if n < N_G - 3 else S_LATE[n - (N_G - 3)]
+            at(u + s_at, tail_s, n)
+            at(u + s_at + V_AT, tail_v, n)
             for k, (b, c0, c1, engs) in enumerate(SQ):
                 if b == ob:
                     for a in range(A):
-                        at(u + S_AT + V_AT + Q_AT + a * Q_STEP // 2, squares, rt, k, c0 * P, c1 * P, a, engs[a])
+                        at(u + s_at + V_AT + Q_AT + a * Q_STEP // 2, squares, rt, k, c0 * P, c1 * P, a, engs[a])
                     if k == len(SQ) - 1:
-                        at(u + S_AT + V_AT + Q_AT + 3 * Q_STEP // 2 + 1, sum_early, rt)
+                        at(u + s_at + V_AT + Q_AT + 3 * Q_STEP // 2 + 1, sum_early, rt)
             if ob == N_OB - 1:
-                at(u + S_AT + N_AT, norm, n)
+                at(u + s_at + N_AT, norm, n)
                 for a in range(A):
-                    at(u + S_AT + max(N_AT, V_AT) + F_AT + a * F_STEP // 2, scale, rt, a, FIN[rt][a])
-                at(u + S_AT + max(N_AT, V_AT) + F_AT + 3 * F_STEP // 2, store, rt, 0, A)
+                    at(u + s_at + max(N_AT, V_AT) + F_AT + a * F_STEP // 2, scale, rt, a, FIN[rt][a])
+                    if STORE[rt] == 1 or a == A - 1 or (STORE[rt] == 2 and a % 2 == 1):
+                        at(u + s_at + max(N_AT, V_AT) + F_AT + a * F_STEP // 2, store, rt, a + 1 - STORE[rt], a + 1)
 
         u_tiles = {}
         prods = {}
@@ -353,7 +362,7 @@ def tile_gnn_new_pb_kernel(tc, h, neighbours, W_node, b_node, W_nb, b_nb, out):
                     if f != tail_t:
                         f(*args)
                 if g == G - 1 and n < N_G - 1:
-                    at(j + 1 + T_AT, tail_t, n, terms)
+                    at(j + 1 + t_at(n), tail_t, n, terms)
         n = N_G - 1
         tail_t(n, terms)
         for u in range(N_U, N_U + 12):

@@ -29,6 +29,8 @@ VLAG = 1
 ADDS = (1, 0, 1, 1, 1, 1, 1, 1, 1, 2, 2, 0)
 T_LATE = (3, 3)
 T_AT = 3
+T_CUT = 0
+T_GAP = 1
 S_AT = 2
 S_LATE = (2, 2)
 V_AT = 1
@@ -38,16 +40,16 @@ N_AT = 2
 F_AT = 1
 F_STEP = 2
 FIN = ('GGVV', 'VVVV', 'VVSV')
-STORE = (1, 1)
-SQ = ((2, 0, 3, 'SSVV'),)
+SQ = ("SSVV", "SSVV", "SSVV")
+SPLIT = False
 W_Q = ((0, 8), (8, 2))
 Q_U = 0
 P_U = 1
-P_ENG = 'GGGGSGGGGS'
+P_ENG = "GGGGSGGGGS" * 3
 PIECES = (5, 5, 4, 3, 3, 4, 3, 3, 0, 0, 0, 0)
-X_T = (0, 1, 2, 3)
+X_T = (0, 0, 1, 1, 2, 2, 3, 3)
 X_Q = (1, 6)
-X_ENG = ('SV', 'SV', 'SV', 'SV')
+X_ENG = "SVSVSSSV"
 HEAD_ENG = ("VVSSS", "VVSSS")
 
 
@@ -76,12 +78,13 @@ def tile_gnn_new_pb_kernel(tc, h, neighbours, W_node, b_node, W_nb, b_nb, out):
         y = [keep.tile([P, A, O], F32, name="y%d" % rt) for rt in range(N_RT)]
         ident = keep.tile([P, P], F32, name="ident")
         ident_b = keep.tile([P, P], BF16, name="ident_b")
+        warm_b = keep.tile([P, 512], BF16, name="warm_b")
         braw = keep.tile([P, CH], BF16, name="braw")
         bias_t = keep.tile([P, G, 2 * N_OB], F32, name="bias_t")
         one = keep.tile([P, 1], F32, name="one")
         warm = keep.tile([P, 1], F32, name="warm")
-        part = [[keep.tile([P, A], F32, name="part%d%d" % (rt, k)) for k in range(len(SQ) + 1)] for rt in range(N_RT)]
-        ssum = [keep.tile([P, A], F32, name="ssum%d" % rt) for rt in range(N_RT)]
+        part = [[keep.tile([P, A], F32, name="part%d%d" % (rt, k)) for k in range(2)] for rt in range(N_RT)]
+        eps = keep.tile([P, 1], F32, name="eps")
         rn = [keep.tile([P, A], F32, name="rn%d" % rt) for rt in range(N_RT)]
 
         ctx.enter_context(tc.manual_schedule())
@@ -100,7 +103,9 @@ def tile_gnn_new_pb_kernel(tc, h, neighbours, W_node, b_node, W_nb, b_nb, out):
                 )
 
         nc.gpsimd.memset(braw[:].bitcast(F32), 0.0)
+        nc.vector.memset(warm_b[:].bitcast(F32), 0.0)
         nc.vector.memset(one[:], 1.0)
+        nc.vector.memset(eps[:], 1.0e-26)
         load_x(0, 0)
         nc.sync.dma_start(out=braw[0:N_OB, :], in_=b_node.rearrange("(o c) -> o c", o=N_OB))
         nc.sync.dma_start(out=braw[N_OB:2 * N_OB, :], in_=b_nb.rearrange("(o c) -> o c", o=N_OB))
@@ -117,6 +122,11 @@ def tile_gnn_new_pb_kernel(tc, h, neighbours, W_node, b_node, W_nb, b_nb, out):
         make_identity(nc, ident_b[:])
         nc.scalar.activation(out=warm[:], in_=one[:], func=ACT.Abs_reciprocal_sqrt)
 
+        def keep_warm(k):
+            bank = pv.tile([P, 512], F32, tag="v")
+            for i in range(k):
+                nc.tensor.matmul(out=bank[:], lhsT=warm_b[:, 0:P], rhs=warm_b[:], start=True, stop=True)
+
         def turn_bias():
             cols = braw[:].rearrange("p (m g) -> p g m", g=G)
             t = pz.tile([P, G, P], BF16, tag="z")
@@ -126,23 +136,26 @@ def tile_gnn_new_pb_kernel(tc, h, neighbours, W_node, b_node, W_nb, b_nb, out):
 
         xg = {}
 
-        def turn_x(x, rt, engines):
-            if x == 0:
+        def turn_half(x, rt, half, engine):
+            if x == 0 and half == 0:
                 grouped = xstage.tile([P, 2, 4 * RT], BF16, tag="xg", align_bytes=64)
                 xg[rt] = grouped
             g32 = xg[rt][:, x, :].bitcast(F32).rearrange("q (a c u) -> q a c u", a=A, u=2)
             r32 = xraw[x][rt][:].bitcast(F32)
+            t = pz.tile([P, 512], F32, tag="z")
+            for i in range(4):
+                col = half * 512 + i * P
+                nc.tensor.transpose(t[:, i * P:(i + 1) * P], r32[:, col:col + P], ident[:])
+            dst = g32[:, 2 * half:2 * half + 2]
+            src = t[:].rearrange("q (a u c) -> q a c u", a=2, u=2)
+            if engine == "S":
+                nc.scalar.copy(out=dst, in_=src)
+            else:
+                nc.vector.tensor_copy(out=dst, in_=src)
+
+        def turn_x(x, rt, engines):
             for half in range(2):
-                t = pz.tile([P, 512], F32, tag="z")
-                for i in range(4):
-                    col = half * 512 + i * P
-                    nc.tensor.transpose(t[:, i * P:(i + 1) * P], r32[:, col:col + P], ident[:])
-                dst = g32[:, 2 * half:2 * half + 2]
-                src = t[:].rearrange("q (a u c) -> q a c u", a=2, u=2)
-                if engines[half] == "S":
-                    nc.scalar.copy(out=dst, in_=src)
-                else:
-                    nc.vector.tensor_copy(out=dst, in_=src)
+                turn_half(x, rt, half, engines[half])
 
         def quant_x(x, k, rt):
             nc.vector.quantize_mx(
@@ -174,76 +187,81 @@ def tile_gnn_new_pb_kernel(tc, h, neighbours, W_node, b_node, W_nb, b_nb, out):
                 in_=wg[ob][:, i0:i0 + k].rearrange("q i m t -> q (i m t)"),
             )
 
-        def one_pass(w, ob, rt, g):
+        groups = [(ob, rt, 0, A) for ob in range(N_OB) for rt in range(N_RT)]
+        if SPLIT:
+            groups[-1:] = [(N_OB - 1, N_RT - 1, 0, 2), (N_OB - 1, N_RT - 1, 2, 2)]
+        N_G = len(groups)
+        N_U = N_G * G
+
+        def one_pass(w, n, g):
+            ob, rt, a0, na = groups[n]
             cols = slice(g * P, (g + 1) * P)
+            rows = slice(a0 * P, (a0 + na) * P)
             pool = pu if w == 0 else pv
-            bank = pool.tile([P, RT], F32, tag="u" if w == 0 else "v")
+            bank = pool.tile([P, na * P], F32, tag="u" if w == 0 else "v")
             nc.tensor.matmul_mx(
                 out=bank[:],
                 lhsT=wc[ob][:, w, cols].bitcast(FP8X4),
                 lhsT_scale=ws[ob][:, w, cols],
-                rhs=xc[rt][:, w, :].bitcast(FP8X4),
-                rhs_scale=xs[rt][:, w, :],
+                rhs=xc[rt][:, w, rows].bitcast(FP8X4),
+                rhs_scale=xs[rt][:, w, rows],
                 start=True,
                 stop=True,
             )
             return bank
 
-        def take_u(ob, g, bank):
-            u_sb = upool.tile([P, RT], F32, tag="usb")
+        def take_u(n, g, bank):
+            ob, rt, a0, na = groups[n]
+            u_sb = upool.tile([P, na * P], F32, tag="usb")
             nc.scalar.activation(out=u_sb[:], in_=bank[:], func=ACT.Identity,
                                  bias=bias_t[:, g, ob:ob + 1], scale=1.0)
             return u_sb
 
-        def product(ob, g, bank, u_sb):
-            prod = ppool.tile([P, RT], F32, tag="p")
+        def product(n, g, bank, u_sb):
+            ob, rt, a0, na = groups[n]
+            prod = ppool.tile([P, na * P], F32, tag="p")
             nc.vector.scalar_tensor_tensor(out=prod[:], in0=bank[:], scalar=bias_t[:, g, N_OB + ob:N_OB + ob + 1],
                                            in1=u_sb[:], op0=ALU.add, op1=ALU.mult)
             return prod
 
-        def add_pair(p0, p1):
-            s = apool.tile([P, RT], F32, tag="s")
+        def add_pair(n, p0, p1):
+            s = apool.tile([P, groups[n][3] * P], F32, tag="s")
             nc.gpsimd.tensor_tensor(out=s[:], in0=p0[:], in1=p1[:], op=ALU.add)
             return s
 
-        def pool_terms(z, terms, first, last):
-            for k, term in enumerate(terms):
-                for a in range(A):
-                    nc.tensor.matmul(out=z[:, a, :], lhsT=term[:, a * P:(a + 1) * P], rhs=ident[:],
-                                     start=(first and k == 0 and a == 0),
-                                     stop=(last and k == len(terms) - 1 and a == A - 1), is_transpose=True)
-
-        N_G = N_OB * N_RT
-        N_U = N_G * G
         side = {}
 
         def at(u, f, *args):
             side.setdefault(u, []).append((f, args))
 
-        def t_at(n):
-            return T_AT if n < N_G - 3 else T_LATE[n - (N_G - 3)]
-
         sums = {}
         roots = {}
 
-        def tail_t(n, terms):
-            z = pz.tile([P, A, P], F32, tag="z")
-            sums[n] = z
-            pool_terms(z, terms, True, True)
+        def tail_t(n, terms, k0, k1):
+            na = groups[n][3]
+            if k0 == 0:
+                z = pz.tile([P, na, P], F32, tag="z")
+                sums[n] = z
+            z = sums[n]
+            for k in range(k0, k1):
+                for a in range(na):
+                    nc.tensor.matmul(out=z[:, a, :], lhsT=terms[k][:, a * P:(a + 1) * P], rhs=ident[:],
+                                     start=(k == 0 and a == 0), stop=(k == len(terms) - 1 and a == na - 1),
+                                     is_transpose=True)
 
         def tail_s(n):
-            w_sb = rpool.tile([P, A, P], F32, tag="w")
+            w_sb = rpool.tile([P, groups[n][3], P], F32, tag="w")
             roots[n] = w_sb
             nc.scalar.activation(out=w_sb[:], in_=sums[n][:], func=ACT.Abs_reciprocal_sqrt)
 
         def tail_v(n):
-            ob, rt = n // N_RT, n % N_RT
-            nc.vector.scalar_tensor_tensor(out=y[rt][:, :, ob * P:(ob + 1) * P], in0=roots[n][:], scalar=BIG,
+            ob, rt, a0, na = groups[n]
+            nc.vector.scalar_tensor_tensor(out=y[rt][:, a0:a0 + na, ob * P:(ob + 1) * P], in0=roots[n][:], scalar=BIG,
                                            in1=sums[n][:], op0=ALU.min, op1=ALU.mult)
 
-        def squares(rt, k, c0, c1, a, eng):
+        def squares(rt, c0, c1, a, eng):
             src = y[rt][:, a, c0:c1]
-            acc = part[rt][k][:, a:a + 1]
+            acc = part[rt][0][:, a:a + 1]
             if eng == "S":
                 junk = rpool.tile([P, O], F32, tag="junk")
                 nc.scalar.activation(out=junk[:, 0:c1 - c0], in_=src, func=ACT.Square, accum_out=acc)
@@ -252,22 +270,15 @@ def tile_gnn_new_pb_kernel(tc, h, neighbours, W_node, b_node, W_nb, b_nb, out):
                 nc.vector.scalar_tensor_tensor(out=junk_v[:, 0:c1 - c0], in0=src, scalar=1.0, in1=src,
                                                op0=ALU.mult, op1=ALU.mult, accum_out=acc)
 
-        def sum_early(rt):
-            total = part[rt][0]
-            if len(SQ) > 1:
-                total = ssum[rt]
-                nc.vector.tensor_tensor(out=total[:], in0=part[rt][0][:], in1=part[rt][1][:], op=ALU.add)
-            nc.vector.tensor_scalar_max(out=ssum[rt][:], in0=total[:], scalar1=1.0e-24)
-
         def norm(n):
-            rt = n % N_RT
-            for a in range(A):
+            ob, rt, a0, na = groups[n]
+            for a in range(na):
                 junk = rpool.tile([P, O], F32, tag="junk")
-                nc.scalar.activation(out=junk[:, 0:P], in_=sums[n][:, a, :], func=ACT.Abs,
-                                     accum_out=part[rt][len(SQ)][:, a:a + 1])
-            for a in range(A):
-                nc.scalar.activation(out=rn[rt][:, a:a + 1], in_=part[rt][len(SQ)][:, a:a + 1],
-                                     func=ACT.Abs_reciprocal_sqrt, bias=ssum[rt][:, a:a + 1])
+                nc.scalar.activation(out=junk[:, 0:P], in_=sums[n][:, a, :], func=ACT.Abs, bias=eps[:],
+                                     accum_out=part[rt][1][:, a0 + a:a0 + a + 1])
+            for a in range(a0, a0 + na):
+                nc.scalar.activation(out=rn[rt][:, a:a + 1], in_=part[rt][1][:, a:a + 1],
+                                     func=ACT.Abs_reciprocal_sqrt, bias=part[rt][0][:, a:a + 1])
 
         out_v = out.rearrange("(t p a) o -> t p a o", t=N_RT, a=A)
 
@@ -281,16 +292,19 @@ def tile_gnn_new_pb_kernel(tc, h, neighbours, W_node, b_node, W_nb, b_nb, out):
             else:
                 nc.vector.tensor_scalar_mul(out=t, in0=t, scalar1=sc)
 
-        def store(rt, a0, a1):
-            nc.sync.dma_start(out=out_v[rt][:, a0:a1], in_=y[rt][:, a0:a1, :])
+        def store(rt, a):
+            nc.sync.dma_start(out=out_v[rt][:, a, :], in_=y[rt][:, a, :])
 
+        keep_warm(5)
         turn_x(0, 0, "VS")
         turn_bias()
+        keep_warm(2)
         for g in range(G):
             regroup_w(0, 0, g, HEAD_ENG[0][g])
         quant_x(0, 1, 0)
         quant_w(0, 0, 1)
         turn_x(1, 0, "VS")
+        keep_warm(1)
         quant_w(0, 1, 4)
         for g in range(G):
             regroup_w(1, 0, g, HEAD_ENG[1][g])
@@ -298,42 +312,41 @@ def tile_gnn_new_pb_kernel(tc, h, neighbours, W_node, b_node, W_nb, b_nb, out):
         quant_w(0, 5, 1)
         quant_w(0, 6, 4)
 
-        for i in range(4):
-            rt, x = 1 + i // 2, i % 2
-            at(X_T[i], turn_x, x, rt, X_ENG[i])
-            if x == 1:
+        for i in range(8):
+            rt, x, half = 1 + i // 4, i // 2 % 2, i % 2
+            at(X_T[i], turn_half, x, rt, half, X_ENG[i])
+            if x == 1 and half == 1:
                 at(X_Q[rt - 1], quant_x, 0, 2, rt)
         q = 0
         done = []
-        for n in range(N_G):
+        for n in range(len(PIECES)):
             for ob in done:
                 for i0, k in W_Q:
                     at(5 * n + Q_U, quant_w, ob, i0, k)
             done = []
             for c in range(PIECES[n]):
                 ob, w, g = 1 + q // 10, q % 10 // G, q % G
-                at(5 * n + P_U, regroup_w, w, ob, g, P_ENG[q % 10])
+                at(5 * n + P_U, regroup_w, w, ob, g, P_ENG[q])
                 if q % 10 == 9:
                     done.append(ob)
                 q += 1
         for n in range(N_G - 1):
-            ob, rt = n // N_RT, n % N_RT
-            u = 5 * n + 5 + t_at(n)
-            s_at = S_AT if n < N_G - 3 else S_LATE[n - (N_G - 3)]
+            ob, rt, a0, na = groups[n]
+            late = max(0, n - (N_G - 1 - len(T_LATE))) if n >= N_G - 1 - len(T_LATE) else None
+            t_at = T_AT if late is None else T_LATE[late]
+            s_at = S_AT if late is None else S_LATE[late]
+            u = 5 * n + 5 + t_at
             at(u + s_at, tail_s, n)
             at(u + s_at + V_AT, tail_v, n)
-            for k, (b, c0, c1, engs) in enumerate(SQ):
-                if b == ob:
-                    for a in range(A):
-                        at(u + s_at + V_AT + Q_AT + a * Q_STEP // 2, squares, rt, k, c0 * P, c1 * P, a, engs[a])
-                    if k == len(SQ) - 1:
-                        at(u + s_at + V_AT + Q_AT + 3 * Q_STEP // 2 + 1, sum_early, rt)
+            if ob == N_OB - 2:
+                for a in range(A):
+                    at(u + s_at + V_AT + Q_AT + a * Q_STEP // 2, squares, rt, 0, 3 * P, a, SQ[rt][a])
             if ob == N_OB - 1:
                 at(u + s_at + N_AT, norm, n)
-                for a in range(A):
-                    at(u + s_at + max(N_AT, V_AT) + F_AT + a * F_STEP // 2, scale, rt, a, FIN[rt][a])
-                    if STORE[rt] == 1 or a == A - 1 or (STORE[rt] == 2 and a % 2 == 1):
-                        at(u + s_at + max(N_AT, V_AT) + F_AT + a * F_STEP // 2, store, rt, a + 1 - STORE[rt], a + 1)
+                for a in range(a0, a0 + na):
+                    v = u + s_at + max(N_AT, V_AT) + F_AT + (a - a0) * F_STEP // 2
+                    at(v, scale, rt, a, FIN[rt][a])
+                    at(v, store, rt, a)
 
         u_tiles = {}
         prods = {}
@@ -341,17 +354,19 @@ def tile_gnn_new_pb_kernel(tc, h, neighbours, W_node, b_node, W_nb, b_nb, out):
         for i in range(N_U + VLAG):
             if i < N_U:
                 n, g = i // G, i % G
-                bank = one_pass(0, n // N_RT, n % N_RT, g)
-                u_tiles[i] = take_u(n // N_RT, g, bank)
+                bank = one_pass(0, n, g)
+                u_tiles[i] = take_u(n, g, bank)
+                if i < 2:
+                    keep_warm(1)
             j = i - VLAG
             if j >= 0:
                 n, g = j // G, j % G
-                bank = one_pass(1, n // N_RT, n % N_RT, g)
-                prods[j] = product(n // N_RT, g, bank, u_tiles[j])
+                bank = one_pass(1, n, g)
+                prods[j] = product(n, g, bank, u_tiles[j])
                 if g == 0:
                     terms = []
                 if (g == 1 and ADDS[n] > 0) or (g == 3 and ADDS[n] > 1):
-                    terms.append(add_pair(prods[j - 1], prods[j]))
+                    terms.append(add_pair(n, prods[j - 1], prods[j]))
                 elif g == 4 or (g >= 2 and ADDS[n] < 2) or ADDS[n] == 0:
                     terms.append(prods[j])
                 first = side.get(j, [])
@@ -362,15 +377,20 @@ def tile_gnn_new_pb_kernel(tc, h, neighbours, W_node, b_node, W_nb, b_nb, out):
                     if f != tail_t:
                         f(*args)
                 if g == G - 1 and n < N_G - 1:
-                    at(j + 1 + t_at(n), tail_t, n, terms)
+                    t_at = T_AT if n < N_G - 1 - len(T_LATE) else T_LATE[n - (N_G - 1 - len(T_LATE))]
+                    cut = len(terms) if T_CUT == 0 else len(terms) - T_CUT
+                    at(j + 1 + t_at - (T_GAP if cut < len(terms) else 0), tail_t, n, terms, 0, cut)
+                    if cut < len(terms):
+                        at(j + 1 + t_at, tail_t, n, terms, cut, len(terms))
         n = N_G - 1
-        tail_t(n, terms)
+        tail_t(n, terms, 0, len(terms))
         for u in range(N_U, N_U + 12):
             for f, args in side.get(u, ()):
                 f(*args)
+        ob, rt, a0, na = groups[n]
         tail_s(n)
         norm(n)
         tail_v(n)
-        for a in range(A):
-            scale(N_RT - 1, a, FIN[N_RT - 1][a])
-            store(N_RT - 1, a, a + 1)
+        for a in range(a0, a0 + na):
+            scale(rt, a, FIN[rt][a])
+            store(rt, a)

@@ -26,27 +26,28 @@ PU = 3
 PV = 3
 PZ = 2
 VLAG = 1
-ADDS = (1, 0, 1, 1, 1, 1, 1, 1, 1, 2, 2, 0)
-T_LATE = (3, 3)
+ADDS = (1, 0, 1, 1, 1, 1, 1, 2, 2, 2, 2, 0)
+T_LATE = (3, 2)
 T_AT = 3
 T_CUT = 0
 T_GAP = 1
 S_AT = 2
-S_LATE = (2, 2)
+S_LATE = (1, 2)
 V_AT = 1
 Q_AT = 2
 Q_STEP = 3
 N_AT = 2
-F_AT = 1
+F_AT = 0
 F_STEP = 2
-FIN = ('GGVV', 'VVVV', 'VVSV')
+FIN = ('GGGV', 'VVVV', 'VVSV')
 SQ = ("SSVV", "SSVV", "SSVV")
 SPLIT = False
+LAST_SIX = ((2, 0), (2, 1), (3, 0), (2, 2), (3, 1), (3, 2))
 W_Q = ((0, 8), (8, 2))
 Q_U = 0
 P_U = 1
-P_ENG = "GGGGSGGGGS" * 3
-PIECES = (5, 5, 4, 3, 3, 4, 3, 3, 0, 0, 0, 0)
+P_ENG = "GGGGSGGGSS" * 3
+PIECES = (5, 5, 4, 4, 4, 4, 4, 0, 0, 0, 0, 0)
 X_T = (0, 0, 1, 1, 2, 2, 3, 3)
 X_Q = (1, 6)
 X_ENG = "SVSVSSSV"
@@ -187,7 +188,7 @@ def tile_gnn_new_pb_kernel(tc, h, neighbours, W_node, b_node, W_nb, b_nb, out):
                 in_=wg[ob][:, i0:i0 + k].rearrange("q i m t -> q (i m t)"),
             )
 
-        groups = [(ob, rt, 0, A) for ob in range(N_OB) for rt in range(N_RT)]
+        groups = [(ob, rt, 0, A) for ob in range(2) for rt in range(N_RT)] + [(ob, rt, 0, A) for ob, rt in LAST_SIX]
         if SPLIT:
             groups[-1:] = [(N_OB - 1, N_RT - 1, 0, 2), (N_OB - 1, N_RT - 1, 2, 2)]
         N_G = len(groups)

@@ -27,19 +27,19 @@ PV = 3
 PZ = 2
 VLAG = 1
 ADDS = (1, 0, 1, 1, 1, 1, 1, 2, 2, 2, 2, 0)
-T_LATE = (3, 2)
+T_LATE = (3, 3)
 T_AT = 3
 T_CUT = 0
 T_GAP = 1
 S_AT = 2
-S_LATE = (1, 2)
+S_LATE = (2, 0)
 V_AT = 1
 Q_AT = 2
 Q_STEP = 3
-N_AT = 2
-F_AT = 0
+N_AT = 3
+F_AT = 1
 F_STEP = 2
-FIN = ('GGGV', 'VVVV', 'VVSV')
+FIN = ('GGGG', 'VVVV', 'VSVS')
 SQ = ("SSVV", "SSVV", "SSVV")
 SPLIT = False
 LAST_SIX = ((2, 0), (2, 1), (3, 0), (2, 2), (3, 1), (3, 2))
@@ -47,7 +47,7 @@ W_Q = ((0, 8), (8, 2))
 Q_U = 0
 P_U = 1
 P_ENG = "GGGGSGGGSS" * 3
-PIECES = (5, 5, 4, 4, 4, 4, 4, 0, 0, 0, 0, 0)
+PIECES = (5, 5, 5, 4, 3, 4, 4, 0, 0, 0, 0, 0)
 X_T = (0, 0, 1, 1, 2, 2, 3, 3)
 X_Q = (1, 6)
 X_ENG = "SVSVSSSV"

@@ -90,10 +90,11 @@ def tile_gnn_new_pb_kernel(tc, h, neighbours, W_node, b_node, W_nb, b_nb, out):
 
         ctx.enter_context(tc.manual_schedule())
 
-        def load_x(x, rt):
+        def load_x(x, rt, a0=0, na=A):
+            rows = acts[x][rt * RT:(rt + 1) * RT, :].rearrange("(p a) k -> p a k", a=A)
             nc.sync.dma_start(
-                out=xraw[x][rt][:],
-                in_=acts[x][rt * RT:(rt + 1) * RT, :].rearrange("(p a) k -> p (a k)", a=A),
+                out=xraw[x][rt][:].rearrange("p (a k) -> p a k", a=A)[:, a0:a0 + na],
+                in_=rows[:, a0:a0 + na],
             )
 
         def load_w(w, ob):
@@ -107,11 +108,13 @@ def tile_gnn_new_pb_kernel(tc, h, neighbours, W_node, b_node, W_nb, b_nb, out):
         nc.vector.memset(warm_b[:].bitcast(F32), 0.0)
         nc.vector.memset(one[:], 1.0)
         nc.vector.memset(eps[:], 1.0e-26)
-        load_x(0, 0)
+        load_x(0, 0, 0, 2)
+        load_x(0, 0, 2, 2)
         nc.sync.dma_start(out=braw[0:N_OB, :], in_=b_node.rearrange("(o c) -> o c", o=N_OB))
         nc.sync.dma_start(out=braw[N_OB:2 * N_OB, :], in_=b_nb.rearrange("(o c) -> o c", o=N_OB))
         load_w(0, 0)
-        load_x(1, 0)
+        load_x(1, 0, 0, 2)
+        load_x(1, 0, 2, 2)
         load_w(1, 0)
         for kind, k in LATER:
             for i in range(2):
@@ -130,10 +133,10 @@ def tile_gnn_new_pb_kernel(tc, h, neighbours, W_node, b_node, W_nb, b_nb, out):
 
         def turn_bias():
             cols = braw[:].rearrange("p (m g) -> p g m", g=G)
-            t = pz.tile([P, G, P], BF16, tag="z")
+            t = pv.tile([P, G, P], BF16, tag="v")
             for g in range(G):
                 nc.tensor.transpose(t[:, g, :], cols[:, g, :], ident_b[:])
-            nc.vector.tensor_copy(out=bias_t[:], in_=t[:, :, 0:2 * N_OB])
+            return t
 
         xg = {}
 
@@ -296,14 +299,15 @@ def tile_gnn_new_pb_kernel(tc, h, neighbours, W_node, b_node, W_nb, b_nb, out):
         def store(rt, a):
             nc.sync.dma_start(out=out_v[rt][:, a, :], in_=y[rt][:, a, :])
 
-        keep_warm(5)
+        keep_warm(4)
         turn_x(0, 0, "VS")
-        turn_bias()
+        bias_bank = turn_bias()
         keep_warm(2)
         for g in range(G):
             regroup_w(0, 0, g, HEAD_ENG[0][g])
         quant_x(0, 1, 0)
         quant_w(0, 0, 1)
+        nc.vector.tensor_copy(out=bias_t[:], in_=bias_bank[:, :, 0:2 * N_OB])
         turn_x(1, 0, "VS")
         keep_warm(1)
         quant_w(0, 1, 4)

@@ -46,12 +46,13 @@ LAST_SIX = ((2, 0), (2, 1), (3, 0), (2, 2), (3, 1), (3, 2))
 W_Q = ((0, 8), (8, 2))
 Q_U = 0
 P_U = 1
-P_ENG = "GGGGSGGGSS" * 3
-PIECES = (5, 5, 5, 4, 3, 4, 4, 0, 0, 0, 0, 0)
+CUT = ((0, 0, 3, 0, 64, "G"), (0, 0, 3, 64, 128, "G"), (0, 3, 5, 0, 128, "G"),
+       (1, 0, 3, 0, 64, "G"), (1, 0, 3, 64, 128, "G"), (1, 3, 5, 0, 128, "S"))
+PIECES = (3, 3, 3, 2, 2, 2, 3, 0, 0, 0, 0, 0)
 X_T = (0, 0, 1, 1, 2, 2, 3, 3)
 X_Q = (1, 6)
 X_ENG = "SVSVSSSV"
-HEAD_ENG = ("VVSSS", "VVSSS")
+HEAD_CUT = ((0, 2, "V"), (2, 5, "S"))
 
 
 def tile_gnn_new_pb_kernel(tc, h, neighbours, W_node, b_node, W_nb, b_nb, out):
@@ -170,12 +171,12 @@ def tile_gnn_new_pb_kernel(tc, h, neighbours, W_node, b_node, W_nb, b_nb, out):
 
         wg = {}
 
-        def regroup_w(w, ob, g, engine):
-            if w == 0 and g == 0:
+        def regroup_w(w, ob, g0, g1, m0, m1, engine):
+            if w == 0 and g0 == 0 and m0 == 0:
                 grouped = wstage.tile([P, 2 * G, P, 4], BF16, tag="wg", align_bytes=64)
                 wg[ob] = grouped
-            dst = wg[ob][:, w * G + g]
-            src = wraw[w][ob][:].rearrange("q t (m g) -> q g m t", g=G)[:, g]
+            dst = wg[ob][:, w * G + g0:w * G + g1, m0:m1].rearrange("q g m t -> q m g t")
+            src = wraw[w][ob][:].rearrange("q t (m g) -> q m g t", g=G)[:, m0:m1, g0:g1]
             if engine == "S":
                 nc.scalar.copy(out=dst, in_=src)
             elif engine == "V":
@@ -303,16 +304,16 @@ def tile_gnn_new_pb_kernel(tc, h, neighbours, W_node, b_node, W_nb, b_nb, out):
         turn_x(0, 0, "VS")
         bias_bank = turn_bias()
         keep_warm(2)
-        for g in range(G):
-            regroup_w(0, 0, g, HEAD_ENG[0][g])
+        for g0, g1, engine in HEAD_CUT:
+            regroup_w(0, 0, g0, g1, 0, P, engine)
         quant_x(0, 1, 0)
         quant_w(0, 0, 1)
         nc.vector.tensor_copy(out=bias_t[:], in_=bias_bank[:, :, 0:2 * N_OB])
         turn_x(1, 0, "VS")
         keep_warm(1)
         quant_w(0, 1, 4)
-        for g in range(G):
-            regroup_w(1, 0, g, HEAD_ENG[1][g])
+        for g0, g1, engine in HEAD_CUT:
+            regroup_w(1, 0, g0, g1, 0, P, engine)
         quant_x(1, 1, 0)
         quant_w(0, 5, 1)
         quant_w(0, 6, 4)
@@ -330,9 +331,10 @@ def tile_gnn_new_pb_kernel(tc, h, neighbours, W_node, b_node, W_nb, b_nb, out):
                     at(5 * n + Q_U, quant_w, ob, i0, k)
             done = []
             for c in range(PIECES[n]):
-                ob, w, g = 1 + q // 10, q % 10 // G, q % G
-                at(5 * n + P_U, regroup_w, w, ob, g, P_ENG[q])
-                if q % 10 == 9:
+                ob = 1 + q // len(CUT)
+                w, g0, g1, m0, m1, engine = CUT[q % len(CUT)]
+                at(5 * n + P_U, regroup_w, w, ob, g0, g1, m0, m1, engine)
+                if q % len(CUT) == len(CUT) - 1:
                     done.append(ob)
                 q += 1
         for n in range(N_G - 1):

@@ -21,13 +21,13 @@ A = RT // P
 CH = P * G
 FLOPS = 2 * 2 * R * D * J
 BIG = 1.0e19
-LATER = (("x", 1), ("w", 1), ("x", 2), ("w", 2), ("w", 3))
+LATER = (("x", 1), ("x", 2), ("w", 1), ("w", 2), ("w", 3))
 PU = 3
 PV = 3
 PZ = 2
 VLAG = 1
 ADDS = (1, 0, 1, 1, 1, 1, 1, 2, 2, 2, 2, 0)
-T_LATE = (3, 3)
+T_LATE = (3, 2)
 T_AT = 3
 T_CUT = 0
 T_GAP = 1
@@ -48,7 +48,7 @@ Q_U = 0
 P_U = 1
 CUT = ((0, 0, 3, 0, 64, "G"), (0, 0, 3, 64, 128, "G"), (0, 3, 5, 0, 128, "G"),
        (1, 0, 3, 0, 64, "G"), (1, 0, 3, 64, 128, "G"), (1, 3, 5, 0, 128, "S"))
-PIECES = (3, 3, 3, 2, 2, 2, 3, 0, 0, 0, 0, 0)
+PIECES = (3, 3, 3, 2, 3, 2, 2, 0, 0, 0, 0, 0)
 X_T = (0, 0, 1, 1, 2, 2, 3, 3)
 X_Q = (1, 6)
 X_ENG = "SVSVSSSV"

@@ -46,9 +46,9 @@ LAST_SIX = ((2, 0), (2, 1), (3, 0), (2, 2), (3, 1), (3, 2))
 W_Q = ((0, 8), (8, 2))
 Q_U = 0
 P_U = 1
-CUT = ((0, 0, 3, 0, 64, "G"), (0, 0, 3, 64, 128, "G"), (0, 3, 5, 0, 128, "G"),
-       (1, 0, 3, 0, 64, "G"), (1, 0, 3, 64, 128, "G"), (1, 3, 5, 0, 128, "S"))
-PIECES = (3, 3, 3, 2, 3, 2, 2, 0, 0, 0, 0, 0)
+CUT = ((0, 0, 4, 0, 64, "G"), (0, 0, 4, 64, 128, "G"), (0, 4, 5, 0, 128, "S"),
+       (1, 0, 4, 0, 64, "G"), (1, 0, 4, 64, 128, "G"), (1, 4, 5, 0, 128, "S"))
+PIECES = (2, 4, 2, 3, 2, 3, 2, 0, 0, 0, 0, 0)
 X_T = (0, 0, 1, 1, 2, 2, 3, 3)
 X_Q = (1, 6)
 X_ENG = "SVSVSSSV"
@@ -175,8 +175,8 @@ def tile_gnn_new_pb_kernel(tc, h, neighbours, W_node, b_node, W_nb, b_nb, out):
             if w == 0 and g0 == 0 and m0 == 0:
                 grouped = wstage.tile([P, 2 * G, P, 4], BF16, tag="wg", align_bytes=64)
                 wg[ob] = grouped
-            dst = wg[ob][:, w * G + g0:w * G + g1, m0:m1].rearrange("q g m t -> q m g t")
-            src = wraw[w][ob][:].rearrange("q t (m g) -> q m g t", g=G)[:, m0:m1, g0:g1]
+            dst = wg[ob][:, w * G + g0:w * G + g1, m0:m1].rearrange("q g m t -> q m t g")
+            src = wraw[w][ob][:].rearrange("q t (m g) -> q m t g", g=G)[:, m0:m1, :, g0:g1]
             if engine == "S":
                 nc.scalar.copy(out=dst, in_=src)
             elif engine == "V":

from contextlib import ExitStack

import concourse.mybir as mybir
from concourse.masks import make_identity

F32 = mybir.dt.float32
BF16 = mybir.dt.bfloat16
U32 = mybir.dt.uint32
U8 = mybir.dt.uint8
FP8X4 = mybir.dt.float8_e4m3fn_x4
ACT = mybir.ActivationFunctionType
ALU = mybir.AluOpType

P = 128
R, D, O, G = 1536, 512, 512, 5
J = O * G
RT = 512
N_RT = R // RT
N_OB = O // P
A = RT // P
CH = P * G
FLOPS = 2 * 2 * R * D * J
BIG = 1.0e19
LATER = (("x", 1), ("x", 2), ("w", 1), ("w", 2), ("w", 3))
PU = 3
PV = 3
PZ = 2
VLAG = 1
ADDS = (1, 0, 1, 1, 1, 1, 1, 2, 2, 2, 2, 0)
T_LATE = (3, 2)
T_AT = 3
T_CUT = 0
T_GAP = 1
S_AT = 2
S_LATE = (2, 0)
V_AT = 1
Q_AT = 2
Q_STEP = 3
N_AT = 3
F_AT = 1
F_STEP = 2
FIN = ('GGGG', 'VVVV', 'VSVS')
SQ = ("SSVV", "SSVV", "SSVV")
SPLIT = False
LAST_SIX = ((2, 0), (2, 1), (3, 0), (2, 2), (3, 1), (3, 2))
W_Q = ((0, 8), (8, 2))
Q_U = 0
P_U = 1
CUT = ((0, 0, 4, 0, 64, "G"), (0, 0, 4, 64, 128, "G"), (0, 4, 5, 0, 128, "S"),
       (1, 0, 4, 0, 64, "G"), (1, 0, 4, 64, 128, "G"), (1, 4, 5, 0, 128, "S"))
PIECES = (2, 4, 2, 3, 2, 3, 2, 0, 0, 0, 0, 0)
X_T = (0, 0, 1, 1, 2, 2, 3, 3)
X_Q = (1, 6)
X_ENG = "SVSVSSSV"
HEAD_CUT = ((0, 2, "V"), (2, 5, "S"))


def tile_gnn_new_pb_kernel(tc, h, neighbours, W_node, b_node, W_nb, b_nb, out):
    nc = tc.nc
    acts = (h, neighbours)
    weights = (W_node, W_nb)
    with ExitStack() as ctx:
        keep = ctx.enter_context(tc.tile_pool(name="keep", bufs=1))
        xstage = ctx.enter_context(tc.tile_pool(name="xstage", bufs=2))
        wstage = ctx.enter_context(tc.tile_pool(name="wstage", bufs=2))
        upool = ctx.enter_context(tc.tile_pool(name="upool", bufs=4 + VLAG))
        ppool = ctx.enter_context(tc.tile_pool(name="ppool", bufs=12))
        apool = ctx.enter_context(tc.tile_pool(name="apool", bufs=4))
        rpool = ctx.enter_context(tc.tile_pool(name="rpool", bufs=2))
        pu = ctx.enter_context(tc.psum_pool(name="pu", bufs=PU))
        pv = ctx.enter_context(tc.psum_pool(name="pv", bufs=PV))
        pz = ctx.enter_context(tc.psum_pool(name="pz", bufs=PZ))

        xraw = [[keep.tile([P, A * D], BF16, name="xraw%d%d" % (x, rt)) for rt in range(N_RT)] for x in range(2)]
        wraw = [[keep.tile([P, 4, CH], BF16, name="wraw%d%d" % (w, ob)) for ob in range(N_OB)] for w in range(2)]
        xc = [keep.tile([P, 2, RT], U32, name="xc%d" % rt, align_bytes=64) for rt in range(N_RT)]
        xs = [keep.tile([P, 2, RT], U8, name="xs%d" % rt, align_bytes=64) for rt in range(N_RT)]
        wc = [keep.tile([P, 2, CH], U32, name="wc%d" % ob, align_bytes=64) for ob in range(N_OB)]
        ws = [keep.tile([P, 2, CH], U8, name="ws%d" % ob, align_bytes=64) for ob in range(N_OB)]
        y = [keep.tile([P, A, O], F32, name="y%d" % rt) for rt in range(N_RT)]
        ident = keep.tile([P, P], F32, name="ident")
        ident_b = keep.tile([P, P], BF16, name="ident_b")
        warm_b = keep.tile([P, 512], BF16, name="warm_b")
        braw = keep.tile([P, CH], BF16, name="braw")
        bias_t = keep.tile([P, G, 2 * N_OB], F32, name="bias_t")
        one = keep.tile([P, 1], F32, name="one")
        warm = keep.tile([P, 1], F32, name="warm")
        part = [[keep.tile([P, A], F32, name="part%d%d" % (rt, k)) for k in range(2)] for rt in range(N_RT)]
        eps = keep.tile([P, 1], F32, name="eps")
        rn = [keep.tile([P, A], F32, name="rn%d" % rt) for rt in range(N_RT)]

        ctx.enter_context(tc.manual_schedule())

        def load_x(x, rt, a0=0, na=A):
            rows = acts[x][rt * RT:(rt + 1) * RT, :].rearrange("(p a) k -> p a k", a=A)
            nc.sync.dma_start(
                out=xraw[x][rt][:].rearrange("p (a k) -> p a k", a=A)[:, a0:a0 + na],
                in_=rows[:, a0:a0 + na],
            )

        def load_w(w, ob):
            for u in range(2):
                nc.sync.dma_start(
                    out=wraw[w][ob][:, 2 * u:2 * u + 2, :],
                    in_=weights[w][256 * u:256 * u + 256, ob * CH:(ob + 1) * CH].rearrange("(q e) c -> q e c", e=2),
                )

        nc.gpsimd.memset(braw[:].bitcast(F32), 0.0)
        nc.vector.memset(warm_b[:].bitcast(F32), 0.0)
        nc.vector.memset(one[:], 1.0)
        nc.vector.memset(eps[:], 1.0e-26)
        load_x(0, 0, 0, 2)
        load_x(0, 0, 2, 2)
        nc.sync.dma_start(out=braw[0:N_OB, :], in_=b_node.rearrange("(o c) -> o c", o=N_OB))
        nc.sync.dma_start(out=braw[N_OB:2 * N_OB, :], in_=b_nb.rearrange("(o c) -> o c", o=N_OB))
        load_w(0, 0)
        load_x(1, 0, 0, 2)
        load_x(1, 0, 2, 2)
        load_w(1, 0)
        for kind, k in LATER:
            for i in range(2):
                if kind == "x":
                    load_x(i, k)
                else:
                    load_w(i, k)
        make_identity(nc, ident[:])
        make_identity(nc, ident_b[:])
        nc.scalar.activation(out=warm[:], in_=one[:], func=ACT.Abs_reciprocal_sqrt)

        def keep_warm(k):
            bank = pv.tile([P, 512], F32, tag="v")
            for i in range(k):
                nc.tensor.matmul(out=bank[:], lhsT=warm_b[:, 0:P], rhs=warm_b[:], start=True, stop=True)

        def turn_bias():
            cols = braw[:].rearrange("p (m g) -> p g m", g=G)
            t = pv.tile([P, G, P], BF16, tag="v")
            for g in range(G):
                nc.tensor.transpose(t[:, g, :], cols[:, g, :], ident_b[:])
            return t

        xg = {}

        def turn_half(x, rt, half, engine):
            if x == 0 and half == 0:
                grouped = xstage.tile([P, 2, 4 * RT], BF16, tag="xg", align_bytes=64)
                xg[rt] = grouped
            g32 = xg[rt][:, x, :].bitcast(F32).rearrange("q (a c u) -> q a c u", a=A, u=2)
            r32 = xraw[x][rt][:].bitcast(F32)
            t = pz.tile([P, 512], F32, tag="z")
            for i in range(4):
                col = half * 512 + i * P
                nc.tensor.transpose(t[:, i * P:(i + 1) * P], r32[:, col:col + P], ident[:])
            dst = g32[:, 2 * half:2 * half + 2]
            src = t[:].rearrange("q (a u c) -> q a c u", a=2, u=2)
            if engine == "S":
                nc.scalar.copy(out=dst, in_=src)
            else:
                nc.vector.tensor_copy(out=dst, in_=src)

        def turn_x(x, rt, engines):
            for half in range(2):
                turn_half(x, rt, half, engines[half])

        def quant_x(x, k, rt):
            nc.vector.quantize_mx(
                out=xc[rt][:, x:x + k, :].rearrange("p x r -> p (x r)").bitcast(FP8X4),
                scales=xs[rt][:, x:x + k, :].rearrange("p x r -> p (x r)"),
                in_=xg[rt][:, x:x + k, :].rearrange("p x r -> p (x r)"),
            )

        wg = {}

        def regroup_w(w, ob, g0, g1, m0, m1, engine):
            if w == 0 and g0 == 0 and m0 == 0:
                grouped = wstage.tile([P, 2 * G, P, 4], BF16, tag="wg", align_bytes=64)
                wg[ob] = grouped
            dst = wg[ob][:, w * G + g0:w * G + g1, m0:m1].rearrange("q g m t -> q m t g")
            src = wraw[w][ob][:].rearrange("q t (m g) -> q m t g", g=G)[:, m0:m1, :, g0:g1]
            if engine == "S":
                nc.scalar.copy(out=dst, in_=src)
            elif engine == "V":
                nc.vector.tensor_copy(out=dst, in_=src)
            else:
                nc.gpsimd.tensor_scalar(out=dst, in0=src, scalar1=1.0, scalar2=0.0, op0=ALU.mult, op1=ALU.add)

        def quant_w(ob, i0, k):
            cols = slice(i0 * P, (i0 + k) * P)
            nc.vector.quantize_mx(
                out=wc[ob][:].rearrange("p w c -> p (w c)")[:, cols].bitcast(FP8X4),
                scales=ws[ob][:].rearrange("p w c -> p (w c)")[:, cols],
                in_=wg[ob][:, i0:i0 + k].rearrange("q i m t -> q (i m t)"),
            )

        groups = [(ob, rt, 0, A) for ob in range(2) for rt in range(N_RT)] + [(ob, rt, 0, A) for ob, rt in LAST_SIX]
        if SPLIT:
            groups[-1:] = [(N_OB - 1, N_RT - 1, 0, 2), (N_OB - 1, N_RT - 1, 2, 2)]
        N_G = len(groups)
        N_U = N_G * G

        def one_pass(w, n, g):
            ob, rt, a0, na = groups[n]
            cols = slice(g * P, (g + 1) * P)
            rows = slice(a0 * P, (a0 + na) * P)
            pool = pu if w == 0 else pv
            bank = pool.tile([P, na * P], F32, tag="u" if w == 0 else "v")
            nc.tensor.matmul_mx(
                out=bank[:],
                lhsT=wc[ob][:, w, cols].bitcast(FP8X4),
                lhsT_scale=ws[ob][:, w, cols],
                rhs=xc[rt][:, w, rows].bitcast(FP8X4),
                rhs_scale=xs[rt][:, w, rows],
                start=True,
                stop=True,
            )
            return bank

        def take_u(n, g, bank):
            ob, rt, a0, na = groups[n]
            u_sb = upool.tile([P, na * P], F32, tag="usb")
            nc.scalar.activation(out=u_sb[:], in_=bank[:], func=ACT.Identity,
                                 bias=bias_t[:, g, ob:ob + 1], scale=1.0)
            return u_sb

        def product(n, g, bank, u_sb):
            ob, rt, a0, na = groups[n]
            prod = ppool.tile([P, na * P], F32, tag="p")
            nc.vector.scalar_tensor_tensor(out=prod[:], in0=bank[:], scalar=bias_t[:, g, N_OB + ob:N_OB + ob + 1],
                                           in1=u_sb[:], op0=ALU.add, op1=ALU.mult)
            return prod

        def add_pair(n, p0, p1):
            s = apool.tile([P, groups[n][3] * P], F32, tag="s")
            nc.gpsimd.tensor_tensor(out=s[:], in0=p0[:], in1=p1[:], op=ALU.add)
            return s

        side = {}

        def at(u, f, *args):
            side.setdefault(u, []).append((f, args))

        sums = {}
        roots = {}

        def tail_t(n, terms, k0, k1):
            na = groups[n][3]
            if k0 == 0:
                z = pz.tile([P, na, P], F32, tag="z")
                sums[n] = z
            z = sums[n]
            for k in range(k0, k1):
                for a in range(na):
                    nc.tensor.matmul(out=z[:, a, :], lhsT=terms[k][:, a * P:(a + 1) * P], rhs=ident[:],
                                     start=(k == 0 and a == 0), stop=(k == len(terms) - 1 and a == na - 1),
                                     is_transpose=True)

        def tail_s(n):
            w_sb = rpool.tile([P, groups[n][3], P], F32, tag="w")
            roots[n] = w_sb
            nc.scalar.activation(out=w_sb[:], in_=sums[n][:], func=ACT.Abs_reciprocal_sqrt)

        def tail_v(n):
            ob, rt, a0, na = groups[n]
            nc.vector.scalar_tensor_tensor(out=y[rt][:, a0:a0 + na, ob * P:(ob + 1) * P], in0=roots[n][:], scalar=BIG,
                                           in1=sums[n][:], op0=ALU.min, op1=ALU.mult)

        def squares(rt, c0, c1, a, eng):
            src = y[rt][:, a, c0:c1]
            acc = part[rt][0][:, a:a + 1]
            if eng == "S":
                junk = rpool.tile([P, O], F32, tag="junk")
                nc.scalar.activation(out=junk[:, 0:c1 - c0], in_=src, func=ACT.Square, accum_out=acc)
            else:
                junk_v = rpool.tile([P, O], F32, tag="junk_v")
                nc.vector.scalar_tensor_tensor(out=junk_v[:, 0:c1 - c0], in0=src, scalar=1.0, in1=src,
                                               op0=ALU.mult, op1=ALU.mult, accum_out=acc)

        def norm(n):
            ob, rt, a0, na = groups[n]
            for a in range(na):
                junk = rpool.tile([P, O], F32, tag="junk")
                nc.scalar.activation(out=junk[:, 0:P], in_=sums[n][:, a, :], func=ACT.Abs, bias=eps[:],
                                     accum_out=part[rt][1][:, a0 + a:a0 + a + 1])
            for a in range(a0, a0 + na):
                nc.scalar.activation(out=rn[rt][:, a:a + 1], in_=part[rt][1][:, a:a + 1],
                                     func=ACT.Abs_reciprocal_sqrt, bias=part[rt][0][:, a:a + 1])

        out_v = out.rearrange("(t p a) o -> t p a o", t=N_RT, a=A)

        def scale(rt, a, eng):
            sc = rn[rt][:, a:a + 1]
            t = y[rt][:, a, :]
            if eng == "S":
                nc.scalar.activation(out=t, in_=t, func=ACT.Copy, scale=sc)
            elif eng == "G":
                nc.gpsimd.tensor_scalar(out=t, in0=t, scalar1=sc, scalar2=0.0, op0=ALU.mult, op1=ALU.add)
            else:
                nc.vector.tensor_scalar_mul(out=t, in0=t, scalar1=sc)

        def store(rt, a):
            nc.sync.dma_start(out=out_v[rt][:, a, :], in_=y[rt][:, a, :])

        keep_warm(4)
        turn_x(0, 0, "VS")
        bias_bank = turn_bias()
        keep_warm(2)
        for g0, g1, engine in HEAD_CUT:
            regroup_w(0, 0, g0, g1, 0, P, engine)
        quant_x(0, 1, 0)
        quant_w(0, 0, 1)
        nc.vector.tensor_copy(out=bias_t[:], in_=bias_bank[:, :, 0:2 * N_OB])
        turn_x(1, 0, "VS")
        keep_warm(1)
        quant_w(0, 1, 4)
        for g0, g1, engine in HEAD_CUT:
            regroup_w(1, 0, g0, g1, 0, P, engine)
        quant_x(1, 1, 0)
        quant_w(0, 5, 1)
        quant_w(0, 6, 4)

        for i in range(8):
            rt, x, half = 1 + i // 4, i // 2 % 2, i % 2
            at(X_T[i], turn_half, x, rt, half, X_ENG[i])
            if x == 1 and half == 1:
                at(X_Q[rt - 1], quant_x, 0, 2, rt)
        q = 0
        done = []
        for n in range(len(PIECES)):
            for ob in done:
                for i0, k in W_Q:
                    at(5 * n + Q_U, quant_w, ob, i0, k)
            done = []
            for c in range(PIECES[n]):
                ob = 1 + q // len(CUT)
                w, g0, g1, m0, m1, engine = CUT[q % len(CUT)]
                at(5 * n + P_U, regroup_w, w, ob, g0, g1, m0, m1, engine)
                if q % len(CUT) == len(CUT) - 1:
                    done.append(ob)
                q += 1
        for n in range(N_G - 1):
            ob, rt, a0, na = groups[n]
            late = max(0, n - (N_G - 1 - len(T_LATE))) if n >= N_G - 1 - len(T_LATE) else None
            t_at = T_AT if late is None else T_LATE[late]
            s_at = S_AT if late is None else S_LATE[late]
            u = 5 * n + 5 + t_at
            at(u + s_at, tail_s, n)
            at(u + s_at + V_AT, tail_v, n)
            if ob == N_OB - 2:
                for a in range(A):
                    at(u + s_at + V_AT + Q_AT + a * Q_STEP // 2, squares, rt, 0, 3 * P, a, SQ[rt][a])
            if ob == N_OB - 1:
                at(u + s_at + N_AT, norm, n)
                for a in range(a0, a0 + na):
                    v = u + s_at + max(N_AT, V_AT) + F_AT + (a - a0) * F_STEP // 2
                    at(v, scale, rt, a, FIN[rt][a])
                    at(v, store, rt, a)

        u_tiles = {}
        prods = {}
        terms = []
        for i in range(N_U + VLAG):
            if i < N_U:
                n, g = i // G, i % G
                bank = one_pass(0, n, g)
                u_tiles[i] = take_u(n, g, bank)
                if i < 2:
                    keep_warm(1)
            j = i - VLAG
            if j >= 0:
                n, g = j // G, j % G
                bank = one_pass(1, n, g)
                prods[j] = product(n, g, bank, u_tiles[j])
                if g == 0:
                    terms = []
                if (g == 1 and ADDS[n] > 0) or (g == 3 and ADDS[n] > 1):
                    terms.append(add_pair(n, prods[j - 1], prods[j]))
                elif g == 4 or (g >= 2 and ADDS[n] < 2) or ADDS[n] == 0:
                    terms.append(prods[j])
                first = side.get(j, [])
                for f, args in first:
                    if f == tail_t:
                        f(*args)
                for f, args in first:
                    if f != tail_t:
                        f(*args)
                if g == G - 1 and n < N_G - 1:
                    t_at = T_AT if n < N_G - 1 - len(T_LATE) else T_LATE[n - (N_G - 1 - len(T_LATE))]
                    cut = len(terms) if T_CUT == 0 else len(terms) - T_CUT
                    at(j + 1 + t_at - (T_GAP if cut < len(terms) else 0), tail_t, n, terms, 0, cut)
                    if cut < len(terms):
                        at(j + 1 + t_at, tail_t, n, terms, cut, len(terms))
        n = N_G - 1
        tail_t(n, terms, 0, len(terms))
        for u in range(N_U, N_U + 12):
            for f, args in side.get(u, ()):
                f(*args)
        ob, rt, a0, na = groups[n]
        tail_s(n)
        norm(n)
        tail_v(n)
        for a in range(a0, a0 + na):
            scale(rt, a, FIN[rt][a])
            store(rt, a)
